import numpy as np
import ml_dtypes


def mxq(x, axis, fmt="e4m3"):
    dtype, down = {"e4m3": (ml_dtypes.float8_e4m3fn, 7), "e5m2": (ml_dtypes.float8_e5m2, 14)}[fmt]
    v = np.moveaxis(np.asarray(x, np.float32).astype(ml_dtypes.bfloat16).astype(np.float64), axis, -1)
    blocks = v.reshape(v.shape[:-1] + (-1, 32))
    amax = np.abs(blocks).max(-1, keepdims=True)
    byte = np.maximum(np.where(amax > 0, np.frexp(amax)[1] - 1 + 127, 0) - down, 1)
    scale = np.exp2(byte - 127.0)
    codes = (blocks / scale).astype(np.float32).astype(dtype).astype(np.float64)
    return np.moveaxis((codes * scale).reshape(v.shape), -1, axis)


WIDE = False


def mx_kscale(k):
    if not WIDE:
        return np.ones(k)
    levels = np.array([10, -10, 5, -5, 0])
    a = np.random.permutation(np.resize(levels, k // 512 * 4)).reshape(k // 512, 4)
    idx = np.arange(k)
    return np.exp2(a[idx // 512, idx % 128 // 32])


BF16 = ml_dtypes.bfloat16


def bf(x):
    return np.asarray(x, np.float32).astype(BF16)


def f64(x):
    return np.asarray(x).astype(np.float64)


E2M1 = np.array([0.0, 0.5, 1.0, 1.5, 2.0, 3.0, 4.0, 6.0, -0.0, -0.5, -1.0, -1.5, -2.0, -3.0, -4.0, -6.0])


def pack_weight(w, fmt):
    k, n = w.shape
    w = f64(bf(w)).reshape(k // 32, 32, n)
    amax = np.abs(w).max(1)
    if fmt == "e4m3":
        byte = np.frexp(amax)[1] - 1 + 127 - 7
    else:
        mant, ex = np.frexp(amax / 6.0)
        byte = np.where(mant > 0.5, ex, ex - 1) + 127
    byte = np.clip(np.where(amax > 0, byte, 1), 1, 254)
    scaled = (w * np.exp2(127.0 - byte)[:, None, :]).reshape(k, n).astype(np.float32)
    by_word = np.ascontiguousarray(scaled.reshape(k // 512, 128, 4, n).transpose(0, 1, 3, 2))
    if fmt == "e4m3":
        words = by_word.astype(ml_dtypes.float8_e4m3fn).view(np.uint8)
    else:
        c = by_word.astype(ml_dtypes.float4_e2m1fn).view(np.uint8) & 0xF
        words = c[..., 0::2] | (c[..., 1::2] << 4)
    return np.ascontiguousarray(words), np.ascontiguousarray(byte.astype(np.uint8).reshape(k // 512, 16, n))


def unpack_weight(words, scales, fmt):
    g, p, n, _ = words.shape
    if fmt == "e4m3":
        vals = np.ascontiguousarray(words).view(ml_dtypes.float8_e4m3fn).astype(np.float64)
    else:
        nib = np.empty((g, p, n, 4), np.uint8)
        nib[..., 0::2] = words & 0xF
        nib[..., 1::2] = words >> 4
        vals = E2M1[nib]
    vals = vals * np.repeat(np.exp2(scales.astype(np.float64) - 127.0), 8, axis=1)[..., None]
    return vals.transpose(0, 1, 3, 2).reshape(g * 512, n)


B, S, E, H, KD, HD, C = 1, 1024, 1024, 8, 128, 256, 512
V = H * HD
EPS = 1e-5
FMT = "e4m3"


def silu(v):
    return v / (1.0 + np.exp(-v))


def setup_inputs():
    s = mx_kscale(E)
    lvl = np.exp2(np.random.uniform(-9.0, 2.0, (B, S, H, 1)))
    x = bf(np.random.standard_normal((B, S, E)) * s)
    wg_words, wg_scales = pack_weight(np.random.standard_normal((E, V)) / np.sqrt(E) / s[:, None], FMT)
    ret = bf(np.random.standard_normal((B, S, H, HD)) * lvl)
    wo_words, wo_scales = pack_weight(np.random.standard_normal((V, E)) * 1.5 / np.sqrt(V), FMT)
    return {"x": x,
            "wg_words": wg_words,
            "wg_scales": wg_scales,
            "ret": ret,
            "wo_words": wo_words,
            "wo_scales": wo_scales}


def reference(x, wg_words, wg_scales, ret, wo_words, wo_scales):
    g = mxq(f64(x), 2, "e4m3") @ unpack_weight(wg_words, wg_scales, FMT)
    r = f64(ret)
    n = r * (1.0 / np.sqrt(np.mean(r * r, axis=-1, keepdims=True) + EPS))
    h = silu(g) * n.reshape(B, S, V)
    return mxq(h, 2, "e4m3") @ unpack_weight(wo_words, wo_scales, FMT)

@@ -1,0 +1,218 @@
+import concourse.mybir as mybir
+from concourse.masks import make_identity
+
+F32 = mybir.dt.float32
+BF16 = mybir.dt.bfloat16
+I32 = mybir.dt.int32
+U32 = mybir.dt.uint32
+U8 = mybir.dt.uint8
+FP8X4 = mybir.dt.float8_e4m3fn_x4
+ACT = mybir.ActivationFunctionType
+ALU = mybir.AluOpType
+
+P = 128
+S, E, V = 1024, 1024, 2048
+HEADS, HEAD_DIM = 8, 256
+EPS = 1e-5
+K_PASS = 512
+N_TILE = 512
+S_TILES = S // P
+X_PASSES = E // K_PASS
+H_PASSES = V // K_PASS
+G_BANKS = V // N_TILE
+OUT_BANKS = E // N_TILE
+WORDS = K_PASS // 2
+HALF = HEADS // 2
+
+FLOPS = 2 * S * E * V + 2 * S * V * E
+
+
+def transpose_two_passes(nc, bank, rows, first_pass, ident):
+    words = rows.bitcast(F32)
+    for g in range(2):
+        start = WORDS * (first_pass + g)
+        for u in range(2):
+            nc.tensor.transpose(bank[:, g, u, :], words[:, start + u : start + WORDS : 2], ident[:])
+
+
+def regroup_two_passes(nc, grouped, bank):
+    nc.vector.tensor_copy(out=grouped.bitcast(F32), in_=bank[:].rearrange("p g u s -> p g s u"))
+
+
+def quantise_two_passes(nc, codes, scales, grouped):
+    nc.vector.quantize_mx(
+        out=codes.rearrange("p g s -> p (g s)").bitcast(FP8X4),
+        scales=scales.rearrange("p g s -> p (g s)"),
+        in_=grouped.rearrange("p g s t -> p (g s t)"),
+    )
+
+
+def tile_retnet_pc_kernel(tc, x, wg_words, wg_scales, ret, wo_words, wo_scales, out):
+    nc = tc.nc
+    x_rows = x.flatten_outer_dims()
+    ret_rows = ret.rearrange("b s h d -> (b s) (h d)")
+    out_rows = out.flatten_outer_dims()
+
+    with tc.tile_pool(name="keep", bufs=1) as keep, tc.tile_pool(name="work", bufs=3) as work, tc.psum_pool(
+        name="psum", bufs=1
+    ) as psum, tc.manual_schedule():
+        wg_planes = keep.tile([P, V], U8, align_bytes=64)
+        wo_planes = keep.tile([P, E], U8, align_bytes=64)
+        nc.vector.memset(wg_planes[:].bitcast(I32), 0)
+        nc.vector.memset(wo_planes[:].bitcast(I32), 0)
+        minus_half = keep.tile([P, HALF], F32)
+        nc.vector.memset(minus_half[:], -0.5)
+        ident = keep.tile([P, P], F32)
+        make_identity(nc, ident[:])
+
+        wg_codes = keep.tile([P, X_PASSES, V], U32, align_bytes=64)
+        wo_codes = keep.tile([P, H_PASSES, E], U32, align_bytes=64)
+        x_sb = [keep.tile([P, E], BF16, name="x_sb%d" % i) for i in range(S_TILES)]
+        ret_sb = [keep.tile([P, V], BF16, name="ret_sb%d" % i) for i in range(S_TILES)]
+
+        def load_planes(planes, scale_rows, passes):
+            for quadrant in range(4):
+                nc.sync.dma_start(
+                    out=planes[32 * quadrant : 32 * quadrant + 4 * passes, :].bitcast(I32),
+                    in_=scale_rows[:, 4 * quadrant : 4 * quadrant + 4, :].bitcast(I32),
+                )
+
+        def load_rows(i):
+            nc.sync.dma_start(out=x_sb[i][:], in_=x_rows[P * i : P * (i + 1), :])
+            nc.sync.dma_start(out=ret_sb[i][:], in_=ret_rows[P * i : P * (i + 1), :])
+
+        load_planes(wg_planes, wg_scales, X_PASSES)
+        load_planes(wo_planes, wo_scales, H_PASSES)
+        load_rows(0)
+        for n in range(G_BANKS):
+            for g in range(X_PASSES):
+                nc.sync.dma_start(
+                    out=wg_codes[:, g, N_TILE * n : N_TILE * (n + 1)].bitcast(I32),
+                    in_=wg_words[g].rearrange("p n t -> p (n t)")[:, 4 * N_TILE * n : 4 * N_TILE * (n + 1)].bitcast(I32),
+                )
+        load_rows(1)
+        for g in range(H_PASSES):
+            nc.sync.dma_start(
+                out=wo_codes[:, g, :].bitcast(I32), in_=wo_words[g].rearrange("p n t -> p (n t)").bitcast(I32)
+            )
+        for i in range(2, S_TILES):
+            load_rows(i)
+
+        x_codes, x_scales, rstd, silu, h_sb, h_grouped, h_codes, h_scales = {}, {}, {}, {}, {}, {}, {}, {}
+
+        def transpose_and_quantise_x(i):
+            bank = psum.tile([P, 2, 2, P], F32, tag="xt")
+            transpose_two_passes(nc, bank, x_sb[i][:], 0, ident)
+            grouped = work.tile([P, X_PASSES, P, 4], BF16, tag="x_grouped", align_bytes=64)
+            regroup_two_passes(nc, grouped[:], bank)
+            x_codes[i] = work.tile([P, X_PASSES, P], U32, tag="x_codes", align_bytes=64, name="x_codes")
+            x_scales[i] = work.tile([P, X_PASSES, P], U8, tag="x_scales", align_bytes=64, name="x_scales")
+            quantise_two_passes(nc, x_codes[i][:], x_scales[i][:], grouped[:])
+
+        def head_statistics(i):
+            mean_sq = work.tile([P, HEADS], F32, tag="mean_sq")
+            shifted = work.tile([P, HEADS], F32, tag="shifted")
+            rstd[i] = work.tile([P, HEADS], F32, tag="rstd", name="rstd")
+            for half in range(2):
+                for head in range(HALF * half, HALF * (half + 1)):
+                    squares = work.tile([P, HEAD_DIM], BF16, tag="squares")
+                    nc.scalar.activation(
+                        out=squares[:],
+                        in_=ret_sb[i][:, HEAD_DIM * head : HEAD_DIM * (head + 1)],
+                        func=ACT.Square,
+                        scale=HEAD_DIM ** -0.5,
+                        accum_out=mean_sq[:, head : head + 1],
+                    )
+                cols = slice(HALF * half, HALF * (half + 1))
+                nc.gpsimd.tensor_scalar(
+                    out=shifted[:, cols], in0=mean_sq[:, cols], scalar1=1.0, scalar2=EPS, op0=ALU.mult, op1=ALU.add
+                )
+                nc.gpsimd.tensor_tensor(out=rstd[i][:, cols], in0=shifted[:, cols], in1=minus_half[:], op=ALU.pow)
+
+        def gate_matmul_and_silu(i):
+            silu[i] = work.tile([P, V], F32, tag="silu", name="silu")
+            for n in range(G_BANKS):
+                cols = slice(N_TILE * n, N_TILE * (n + 1))
+                acc = psum.tile([P, N_TILE], F32, tag="g", bufs=3)
+                for g in range(X_PASSES):
+                    nc.tensor.matmul_mx(
+                        out=acc[:],
+                        lhsT=x_codes[i][:, g, :].bitcast(FP8X4),
+                        lhsT_scale=x_scales[i][:, g, :],
+                        rhs=wg_codes[:, g, cols].bitcast(FP8X4),
+                        rhs_scale=wg_planes[4 * g : P, cols],
+                        start=(g == 0),
+                        stop=(g == X_PASSES - 1),
+                    )
+                nc.scalar.activation(out=silu[i][:, cols], in_=acc[:], func=ACT.Silu)
+
+        def gate_times_norm(i):
+            h_sb[i] = work.tile([P, V], BF16, tag="h_sb", name="h_sb")
+            for head in range(HEADS):
+                cols = slice(HEAD_DIM * head, HEAD_DIM * (head + 1))
+                nc.vector.scalar_tensor_tensor(
+                    out=h_sb[i][:, cols],
+                    in0=silu[i][:, cols],
+                    scalar=rstd[i][:, head : head + 1],
+                    in1=ret_sb[i][:, cols],
+                    op0=ALU.mult,
+                    op1=ALU.mult,
+                )
+
+        def transpose_h(i):
+            h_grouped[i] = work.tile([P, H_PASSES, P, 4], BF16, tag="h_grouped", align_bytes=64, name="h_grouped")
+            for first in range(0, H_PASSES, 2):
+                bank = psum.tile([P, 2, 2, P], F32, tag="ht", bufs=2)
+                transpose_two_passes(nc, bank, h_sb[i][:], first, ident)
+                regroup_two_passes(nc, h_grouped[i][:, first : first + 2], bank)
+
+        def quantise_h(i):
+            h_codes[i] = work.tile([P, H_PASSES, P], U32, tag="h_codes", align_bytes=64, name="h_codes")
+            h_scales[i] = work.tile([P, H_PASSES, P], U8, tag="h_scales", align_bytes=64, name="h_scales")
+            for first in range(0, H_PASSES, 2):
+                two = slice(first, first + 2)
+                quantise_two_passes(nc, h_codes[i][:, two], h_scales[i][:, two], h_grouped[i][:, two])
+
+        def out_matmul(i):
+            banks = []
+            for n in range(OUT_BANKS):
+                cols = slice(N_TILE * n, N_TILE * (n + 1))
+                acc = psum.tile([P, N_TILE], F32, tag="o", bufs=2)
+                for g in range(H_PASSES):
+                    nc.tensor.matmul_mx(
+                        out=acc[:],
+                        lhsT=h_codes[i][:, g, :].bitcast(FP8X4),
+                        lhsT_scale=h_scales[i][:, g, :],
+                        rhs=wo_codes[:, g, cols].bitcast(FP8X4),
+                        rhs_scale=wo_planes[4 * g : P, cols],
+                        start=(g == 0),
+                        stop=(g == H_PASSES - 1),
+                    )
+                banks.append(acc)
+            return banks
+
+        def store_out(i, banks):
+            for n in range(OUT_BANKS):
+                result = work.tile([P, N_TILE], F32, tag="result", bufs=4)
+                nc.scalar.copy(out=result[:], in_=banks[n][:])
+                nc.sync.dma_start(out=out_rows[P * i : P * (i + 1), N_TILE * n : N_TILE * (n + 1)], in_=result[:])
+
+        transpose_and_quantise_x(0)
+        head_statistics(0)
+        for r in range(S_TILES + 2):
+            banks = None
+            if r < S_TILES:
+                gate_matmul_and_silu(r)
+            if r >= 2:
+                banks = out_matmul(r - 2)
+            if r < S_TILES:
+                gate_times_norm(r)
+            if 1 <= r <= S_TILES:
+                quantise_h(r - 1)
+            if r + 1 < S_TILES:
+                head_statistics(r + 1)
+                transpose_and_quantise_x(r + 1)
+            if r < S_TILES:
+                transpose_h(r)
+            if r >= 2:
+                store_out(r - 2, banks)

@@ -35,8 +35,8 @@ def transpose_two_passes(nc, bank, rows, first_pass, ident):
             nc.tensor.transpose(bank[:, g, u, :], words[:, start + u : start + WORDS : 2], ident[:])
 
 
-def regroup_two_passes(nc, grouped, bank):
-    nc.vector.tensor_copy(out=grouped.bitcast(F32), in_=bank[:].rearrange("p g u s -> p g s u"))
+def regroup_two_passes(copy, grouped, bank):
+    copy(out=grouped.bitcast(F32), in_=bank[:].rearrange("p g u s -> p g s u"))
 
 
 def quantise_two_passes(nc, codes, scales, grouped):
@@ -58,13 +58,6 @@ def tile_retnet_pc_kernel(tc, x, wg_words, wg_scales, ret, wo_words, wo_scales, 
     ) as psum, tc.manual_schedule():
         wg_planes = keep.tile([P, V], U8, align_bytes=64)
         wo_planes = keep.tile([P, E], U8, align_bytes=64)
-        nc.vector.memset(wg_planes[:].bitcast(I32), 0)
-        nc.vector.memset(wo_planes[:].bitcast(I32), 0)
-        minus_half = keep.tile([P, HALF], F32)
-        nc.vector.memset(minus_half[:], -0.5)
-        ident = keep.tile([P, P], F32)
-        make_identity(nc, ident[:])
-
         wg_codes = keep.tile([P, X_PASSES, V], U32, align_bytes=64)
         wo_codes = keep.tile([P, H_PASSES, E], U32, align_bytes=64)
         x_sb = [keep.tile([P, E], BF16, name="x_sb%d" % i) for i in range(S_TILES)]
@@ -77,78 +70,118 @@ def tile_retnet_pc_kernel(tc, x, wg_words, wg_scales, ret, wo_words, wo_scales, 
                     in_=scale_rows[:, 4 * quadrant : 4 * quadrant + 4, :].bitcast(I32),
                 )
 
-        def load_rows(i):
+        def load_x(i):
             nc.sync.dma_start(out=x_sb[i][:], in_=x_rows[P * i : P * (i + 1), :])
+
+        def load_ret(i):
             nc.sync.dma_start(out=ret_sb[i][:], in_=ret_rows[P * i : P * (i + 1), :])
 
+        load_x(0)
+        nc.vector.memset(wg_planes[:].bitcast(I32), 0)
+        nc.vector.memset(wo_planes[:].bitcast(I32), 0)
+        minus_half = keep.tile([P, HEADS], F32)
+        nc.vector.memset(minus_half[:], -0.5)
+        ident = keep.tile([P, P], F32)
+        make_identity(nc, ident[:])
+        warm = keep.tile([P, 1], F32)
+        nc.scalar.activation(out=warm[:], in_=minus_half[:, 0:1], func=ACT.Silu)
         load_planes(wg_planes, wg_scales, X_PASSES)
-        load_planes(wo_planes, wo_scales, H_PASSES)
-        load_rows(0)
+        load_x(1)
+        load_ret(0)
         for n in range(G_BANKS):
             for g in range(X_PASSES):
                 nc.sync.dma_start(
                     out=wg_codes[:, g, N_TILE * n : N_TILE * (n + 1)].bitcast(I32),
                     in_=wg_words[g].rearrange("p n t -> p (n t)")[:, 4 * N_TILE * n : 4 * N_TILE * (n + 1)].bitcast(I32),
                 )
-        load_rows(1)
+        load_x(2)
+        load_ret(1)
+        load_ret(2)
+        load_x(3)
+        load_planes(wo_planes, wo_scales, H_PASSES)
         for g in range(H_PASSES):
             nc.sync.dma_start(
                 out=wo_codes[:, g, :].bitcast(I32), in_=wo_words[g].rearrange("p n t -> p (n t)").bitcast(I32)
             )
-        for i in range(2, S_TILES):
-            load_rows(i)
+        load_ret(3)
+        for i in range(4, S_TILES):
+            load_x(i)
+            load_ret(i)
 
-        x_codes, x_scales, rstd, silu, h_sb, h_grouped, h_codes, h_scales = {}, {}, {}, {}, {}, {}, {}, {}
+        x_bank, x_grouped, x_codes, x_scales = {}, {}, {}, {}
+        mean_sq, rstd, silu, h_sb = {}, {}, {}, {}
+        h_banks, h_grouped, h_codes, h_scales, out_banks = {}, {}, {}, {}, {}
 
-        def transpose_and_quantise_x(i):
-            bank = psum.tile([P, 2, 2, P], F32, tag="xt")
-            transpose_two_passes(nc, bank, x_sb[i][:], 0, ident)
-            grouped = work.tile([P, X_PASSES, P, 4], BF16, tag="x_grouped", align_bytes=64)
-            regroup_two_passes(nc, grouped[:], bank)
+        def transpose_x(i):
+            x_bank[i] = psum.tile([P, 2, 2, P], F32, tag="xt", name="xt")
+            transpose_two_passes(nc, x_bank[i], x_sb[i][:], 0, ident)
+
+        def regroup_x(i):
+            x_grouped[i] = work.tile([P, X_PASSES, P, 4], BF16, tag="x_grouped", align_bytes=64, name="x_grouped")
+            regroup_two_passes(nc.vector.tensor_copy, x_grouped[i][:], x_bank[i])
+
+        def quantise_x(i):
             x_codes[i] = work.tile([P, X_PASSES, P], U32, tag="x_codes", align_bytes=64, name="x_codes")
             x_scales[i] = work.tile([P, X_PASSES, P], U8, tag="x_scales", align_bytes=64, name="x_scales")
-            quantise_two_passes(nc, x_codes[i][:], x_scales[i][:], grouped[:])
+            quantise_two_passes(nc, x_codes[i][:], x_scales[i][:], x_grouped[i][:])
 
-        def head_statistics(i):
-            mean_sq = work.tile([P, HEADS], F32, tag="mean_sq")
-            shifted = work.tile([P, HEADS], F32, tag="shifted")
-            rstd[i] = work.tile([P, HEADS], F32, tag="rstd", name="rstd")
-            for half in range(2):
-                for head in range(HALF * half, HALF * (half + 1)):
-                    squares = work.tile([P, HEAD_DIM], BF16, tag="squares")
-                    nc.scalar.activation(
-                        out=squares[:],
-                        in_=ret_sb[i][:, HEAD_DIM * head : HEAD_DIM * (head + 1)],
-                        func=ACT.Square,
-                        scale=HEAD_DIM ** -0.5,
-                        accum_out=mean_sq[:, head : head + 1],
-                    )
-                cols = slice(HALF * half, HALF * (half + 1))
-                nc.gpsimd.tensor_scalar(
-                    out=shifted[:, cols], in0=mean_sq[:, cols], scalar1=1.0, scalar2=EPS, op0=ALU.mult, op1=ALU.add
+        def open_statistics(i):
+            mean_sq[i] = work.tile([P, HEADS], F32, tag="mean_sq", name="mean_sq")
+
+        def mean_square_on_scalar(i, heads):
+            for head in heads:
+                squares = work.tile([P, HEAD_DIM], BF16, tag="squares")
+                nc.scalar.activation(
+                    out=squares[:],
+                    in_=ret_sb[i][:, HEAD_DIM * head : HEAD_DIM * (head + 1)],
+                    func=ACT.Square,
+                    scale=HEAD_DIM ** -0.5,
+                    accum_out=mean_sq[i][:, head : head + 1],
                 )
-                nc.gpsimd.tensor_tensor(out=rstd[i][:, cols], in0=shifted[:, cols], in1=minus_half[:], op=ALU.pow)
 
-        def gate_matmul_and_silu(i):
-            silu[i] = work.tile([P, V], F32, tag="silu", name="silu")
-            for n in range(G_BANKS):
-                cols = slice(N_TILE * n, N_TILE * (n + 1))
-                acc = psum.tile([P, N_TILE], F32, tag="g", bufs=3)
-                for g in range(X_PASSES):
-                    nc.tensor.matmul_mx(
-                        out=acc[:],
-                        lhsT=x_codes[i][:, g, :].bitcast(FP8X4),
-                        lhsT_scale=x_scales[i][:, g, :],
-                        rhs=wg_codes[:, g, cols].bitcast(FP8X4),
-                        rhs_scale=wg_planes[4 * g : P, cols],
-                        start=(g == 0),
-                        stop=(g == X_PASSES - 1),
-                    )
-                nc.scalar.activation(out=silu[i][:, cols], in_=acc[:], func=ACT.Silu)
+        def mean_square_on_vector(i, heads):
+            for head in heads:
+                squares = work.tile([P, HEAD_DIM], BF16, tag="squares_v")
+                cols = slice(HEAD_DIM * head, HEAD_DIM * (head + 1))
+                nc.vector.scalar_tensor_tensor(
+                    out=squares[:],
+                    in0=ret_sb[i][:, cols],
+                    scalar=1.0 / HEAD_DIM,
+                    in1=ret_sb[i][:, cols],
+                    op0=ALU.mult,
+                    op1=ALU.mult,
+                    accum_out=mean_sq[i][:, head : head + 1],
+                )
 
-        def gate_times_norm(i):
-            h_sb[i] = work.tile([P, V], BF16, tag="h_sb", name="h_sb")
-            for head in range(HEADS):
+        def inverse_root(i, first=0, count=HEADS):
+            cols = slice(first, first + count)
+            shifted = work.tile([P, HEADS], F32, tag="shifted")
+            nc.vector.tensor_scalar(out=shifted[:, cols], in0=mean_sq[i][:, cols], scalar1=EPS, scalar2=None, op0=ALU.add)
+            if i not in rstd:
+                rstd[i] = work.tile([P, HEADS], F32, tag="rstd", name="rstd")
+            nc.gpsimd.tensor_tensor(out=rstd[i][:, cols], in0=shifted[:, cols], in1=minus_half[:, cols], op=ALU.pow)
+
+        def gate_matmul(i, n):
+            cols = slice(N_TILE * n, N_TILE * (n + 1))
+            acc = psum.tile([P, N_TILE], F32, tag="g", bufs=3)
+            for g in range(X_PASSES):
+                nc.tensor.matmul_mx(
+                    out=acc[:],
+                    lhsT=x_codes[i][:, g, :].bitcast(FP8X4),
+                    lhsT_scale=x_scales[i][:, g, :],
+                    rhs=wg_codes[:, g, cols].bitcast(FP8X4),
+                    rhs_scale=wg_planes[4 * g : P, cols],
+                    start=(g == 0),
+                    stop=(g == X_PASSES - 1),
+                )
+            if n == 0:
+                silu[i] = work.tile([P, V], F32, tag="silu", name="silu")
+            nc.scalar.activation(out=silu[i][:, cols], in_=acc[:], func=ACT.Silu)
+
+        def gate_times_norm(i, heads):
+            if i not in h_sb:
+                h_sb[i] = work.tile([P, V], BF16, tag="h_sb", name="h_sb")
+            for head in heads:
                 cols = slice(HEAD_DIM * head, HEAD_DIM * (head + 1))
                 nc.vector.scalar_tensor_tensor(
                     out=h_sb[i][:, cols],
@@ -159,60 +192,114 @@ def tile_retnet_pc_kernel(tc, x, wg_words, wg_scales, ret, wo_words, wo_scales, 
                     op1=ALU.mult,
                 )
 
-        def transpose_h(i):
-            h_grouped[i] = work.tile([P, H_PASSES, P, 4], BF16, tag="h_grouped", align_bytes=64, name="h_grouped")
-            for first in range(0, H_PASSES, 2):
-                bank = psum.tile([P, 2, 2, P], F32, tag="ht", bufs=2)
-                transpose_two_passes(nc, bank, h_sb[i][:], first, ident)
-                regroup_two_passes(nc, h_grouped[i][:, first : first + 2], bank)
+        def transpose_h(i, half):
+            h_banks[i, half] = psum.tile([P, 2, 2, P], F32, tag="ht", bufs=2, name="ht")
+            transpose_two_passes(nc, h_banks[i, half], h_sb[i][:], 2 * half, ident)
 
-        def quantise_h(i):
-            h_codes[i] = work.tile([P, H_PASSES, P], U32, tag="h_codes", align_bytes=64, name="h_codes")
-            h_scales[i] = work.tile([P, H_PASSES, P], U8, tag="h_scales", align_bytes=64, name="h_scales")
-            for first in range(0, H_PASSES, 2):
-                two = slice(first, first + 2)
-                quantise_two_passes(nc, h_codes[i][:, two], h_scales[i][:, two], h_grouped[i][:, two])
+        def regroup_h(i, half, copy=nc.vector.tensor_copy):
+            if i not in h_grouped:
+                h_grouped[i] = work.tile([P, H_PASSES, P, 4], BF16, tag="h_grouped", align_bytes=64, name="h_grouped")
+            regroup_two_passes(copy, h_grouped[i][:, 2 * half : 2 * half + 2], h_banks[i, half])
 
-        def out_matmul(i):
-            banks = []
+        def quantise_h(i, half):
+            if i not in h_codes:
+                h_codes[i] = work.tile([P, H_PASSES, P], U32, tag="h_codes", bufs=4, align_bytes=64, name="h_codes")
+                h_scales[i] = work.tile([P, H_PASSES, P], U8, tag="h_scales", bufs=4, align_bytes=64, name="h_scales")
+            two = slice(2 * half, 2 * half + 2)
+            quantise_two_passes(nc, h_codes[i][:, two], h_scales[i][:, two], h_grouped[i][:, two])
+
+        def out_matmul(i, n, passes=range(H_PASSES)):
+            cols = slice(N_TILE * n, N_TILE * (n + 1))
+            if (i, n) not in out_banks:
+                out_banks[i, n] = psum.tile([P, N_TILE], F32, tag="o", bufs=2, name="o")
+            for g in passes:
+                nc.tensor.matmul_mx(
+                    out=out_banks[i, n][:],
+                    lhsT=h_codes[i][:, g, :].bitcast(FP8X4),
+                    lhsT_scale=h_scales[i][:, g, :],
+                    rhs=wo_codes[:, g, cols].bitcast(FP8X4),
+                    rhs_scale=wo_planes[4 * g : P, cols],
+                    start=(g == 0),
+                    stop=(g == H_PASSES - 1),
+                )
+
+        def store_out(i, n, copy=nc.scalar.copy):
+            result = work.tile([P, N_TILE], F32, tag="result", bufs=4)
+            copy(out=result[:], in_=out_banks[i, n][:])
+            nc.sync.dma_start(out=out_rows[P * i : P * (i + 1), N_TILE * n : N_TILE * (n + 1)], in_=result[:])
+
+        on_vector = 1
+        last = S_TILES - 1
+        transpose_x(0)
+        regroup_x(0)
+        transpose_x(1)
+        quantise_x(0)
+        open_statistics(0)
+        mean_square_on_scalar(0, range(HALF))
+        regroup_x(1)
+        mean_square_on_vector(0, range(HALF, HEADS))
+        inverse_root(0, 0, HALF)
+        quantise_x(1)
+        inverse_root(0, HALF, HALF)
+        for n in range(G_BANKS):
+            gate_matmul(0, n)
+            gate_matmul(1, n)
+            gate_times_norm(0, (2 * n, 2 * n + 1))
+        transpose_x(2)
+        regroup_x(2)
+        open_statistics(1)
+        mean_square_on_scalar(1, range(HALF))
+        mean_square_on_vector(1, range(HALF, HEADS))
+        quantise_x(2)
+        inverse_root(1)
+        open_statistics(2)
+        mean_square_on_scalar(2, range(on_vector, HEADS))
+        mean_square_on_vector(2, range(on_vector))
+        for r in range(2, S_TILES):
+            ahead = r + 1 < S_TILES
+            if ahead:
+                transpose_x(r + 1)
+            transpose_h(r - 2, 0)
+            transpose_h(r - 2, 1)
+            inverse_root(r)
+            if ahead:
+                open_statistics(r + 1)
+                regroup_x(r + 1)
+                mean_square_on_vector(r + 1, range(on_vector))
+                quantise_x(r + 1)
+                mean_square_on_scalar(r + 1, range(on_vector, HALF))
+            regroup_h(r - 2, 0)
+            regroup_h(r - 2, 1)
+            quantise_h(r - 2, 0)
+            quantise_h(r - 2, 1)
+            for n in range(G_BANKS):
+                gate_matmul(r, n)
             for n in range(OUT_BANKS):
-                cols = slice(N_TILE * n, N_TILE * (n + 1))
-                acc = psum.tile([P, N_TILE], F32, tag="o", bufs=2)
-                for g in range(H_PASSES):
-                    nc.tensor.matmul_mx(
-                        out=acc[:],
-                        lhsT=h_codes[i][:, g, :].bitcast(FP8X4),
-                        lhsT_scale=h_scales[i][:, g, :],
-                        rhs=wo_codes[:, g, cols].bitcast(FP8X4),
-                        rhs_scale=wo_planes[4 * g : P, cols],
-                        start=(g == 0),
-                        stop=(g == H_PASSES - 1),
-                    )
-                banks.append(acc)
-            return banks
-
-        def store_out(i, banks):
+                out_matmul(r - 2, n)
+            gate_times_norm(r - 1, range(HEADS))
+            if ahead:
+                mean_square_on_scalar(r + 1, range(HALF, HEADS))
             for n in range(OUT_BANKS):
-                result = work.tile([P, N_TILE], F32, tag="result", bufs=4)
-                nc.scalar.copy(out=result[:], in_=banks[n][:])
-                nc.sync.dma_start(out=out_rows[P * i : P * (i + 1), N_TILE * n : N_TILE * (n + 1)], in_=result[:])
-
-        transpose_and_quantise_x(0)
-        head_statistics(0)
-        for r in range(S_TILES + 2):
-            banks = None
-            if r < S_TILES:
-                gate_matmul_and_silu(r)
-            if r >= 2:
-                banks = out_matmul(r - 2)
-            if r < S_TILES:
-                gate_times_norm(r)
-            if 1 <= r <= S_TILES:
-                quantise_h(r - 1)
-            if r + 1 < S_TILES:
-                head_statistics(r + 1)
-                transpose_and_quantise_x(r + 1)
-            if r < S_TILES:
-                transpose_h(r)
-            if r >= 2:
-                store_out(r - 2, banks)
+                store_out(r - 2, n)
+        for half in range(2):
+            transpose_h(last - 1, half)
+            regroup_h(last - 1, half, nc.scalar.copy)
+        gate_times_norm(last, range(HALF))
+        quantise_h(last - 1, 0)
+        quantise_h(last - 1, 1)
+        gate_times_norm(last, range(HALF, HEADS))
+        transpose_h(last, 0)
+        regroup_h(last, 0, nc.scalar.copy)
+        for n in range(OUT_BANKS):
+            out_matmul(last - 1, n)
+        quantise_h(last, 0)
+        transpose_h(last, 1)
+        regroup_h(last, 1)
+        quantise_h(last, 1)
+        for n in range(OUT_BANKS):
+            store_out(last - 1, n)
+        for passes in (range(0, 2), range(2, H_PASSES)):
+            for n in range(OUT_BANKS):
+                out_matmul(last, n, passes)
+        store_out(last, 0)
+        store_out(last, 1, nc.vector.tensor_copy)

@@ -27,12 +27,12 @@ HALF = HEADS // 2
 FLOPS = 2 * S * E * V + 2 * S * V * E
 
 
-def transpose_two_passes(nc, bank, rows, first_pass, ident):
-    words = rows.bitcast(F32)
+def transpose_two_passes(nc, bank, words, first_pass, ident, word_step):
     for g in range(2):
         start = WORDS * (first_pass + g)
         for u in range(2):
-            nc.tensor.transpose(bank[:, g, u, :], words[:, start + u : start + WORDS : 2], ident[:])
+            first = start + (u if word_step == 2 else P * u)
+            nc.tensor.transpose(bank[:, g, u, :], words[:, first : first + word_step * (P - 1) + 1 : word_step], ident[:])
 
 
 def regroup_two_passes(copy, grouped, bank):
@@ -95,9 +95,9 @@ def tile_retnet_pc_kernel(tc, x, wg_words, wg_scales, ret, wo_words, wo_scales, 
                     in_=wg_words[g].rearrange("p n t -> p (n t)")[:, 4 * N_TILE * n : 4 * N_TILE * (n + 1)].bitcast(I32),
                 )
         load_x(2)
+        load_x(3)
         load_ret(1)
         load_ret(2)
-        load_x(3)
         load_planes(wo_planes, wo_scales, H_PASSES)
         for g in range(H_PASSES):
             nc.sync.dma_start(
@@ -114,7 +114,7 @@ def tile_retnet_pc_kernel(tc, x, wg_words, wg_scales, ret, wo_words, wo_scales, 
 
         def transpose_x(i):
             x_bank[i] = psum.tile([P, 2, 2, P], F32, tag="xt", name="xt")
-            transpose_two_passes(nc, x_bank[i], x_sb[i][:], 0, ident)
+            transpose_two_passes(nc, x_bank[i], x_sb[i][:].bitcast(F32), 0, ident, 2)
 
         def regroup_x(i):
             x_grouped[i] = work.tile([P, X_PASSES, P, 4], BF16, tag="x_grouped", align_bytes=64, name="x_grouped")
@@ -183,18 +183,22 @@ def tile_retnet_pc_kernel(tc, x, wg_words, wg_scales, ret, wo_words, wo_scales, 
                 h_sb[i] = work.tile([P, V], BF16, tag="h_sb", name="h_sb")
             for head in heads:
                 cols = slice(HEAD_DIM * head, HEAD_DIM * (head + 1))
-                nc.vector.scalar_tensor_tensor(
-                    out=h_sb[i][:, cols],
-                    in0=silu[i][:, cols],
-                    scalar=rstd[i][:, head : head + 1],
-                    in1=ret_sb[i][:, cols],
-                    op0=ALU.mult,
-                    op1=ALU.mult,
-                )
+                silu_words = silu[i][:, cols].rearrange("s (p u e) -> s u p e", u=2, e=2)
+                ret_words = ret_sb[i][:, cols].rearrange("s (p u e) -> s u p e", u=2, e=2)
+                for u in range(2):
+                    start = K_PASS * (head // 2) + HEAD_DIM * u + P * (head % 2)
+                    nc.vector.scalar_tensor_tensor(
+                        out=h_sb[i][:, start : start + P].rearrange("s (p e) -> s p e", e=2),
+                        in0=silu_words[:, u],
+                        scalar=rstd[i][:, head : head + 1],
+                        in1=ret_words[:, u],
+                        op0=ALU.mult,
+                        op1=ALU.mult,
+                    )
 
         def transpose_h(i, half):
             h_banks[i, half] = psum.tile([P, 2, 2, P], F32, tag="ht", bufs=2, name="ht")
-            transpose_two_passes(nc, h_banks[i, half], h_sb[i][:], 2 * half, ident)
+            transpose_two_passes(nc, h_banks[i, half], h_sb[i][:].bitcast(F32), 2 * half, ident, 1)
 
         def regroup_h(i, half, copy=nc.vector.tensor_copy):
             if i not in h_grouped:
@@ -242,43 +246,46 @@ def tile_retnet_pc_kernel(tc, x, wg_words, wg_scales, ret, wo_words, wo_scales, 
         quantise_x(1)
         inverse_root(0, HALF, HALF)
         for n in range(G_BANKS):
+            if n == G_BANKS - 1:
+                transpose_x(2)
             gate_matmul(0, n)
             gate_matmul(1, n)
-            gate_times_norm(0, (2 * n, 2 * n + 1))
-        transpose_x(2)
-        regroup_x(2)
+            gate_times_norm(0, (2 * n,))
+            if n == G_BANKS - 1:
+                regroup_x(2)
+            gate_times_norm(0, (2 * n + 1,))
+        quantise_x(2)
         open_statistics(1)
         mean_square_on_scalar(1, range(HALF))
         mean_square_on_vector(1, range(HALF, HEADS))
-        quantise_x(2)
         inverse_root(1)
         open_statistics(2)
         mean_square_on_scalar(2, range(on_vector, HEADS))
         mean_square_on_vector(2, range(on_vector))
         for r in range(2, S_TILES):
             ahead = r + 1 < S_TILES
-            if ahead:
-                transpose_x(r + 1)
             transpose_h(r - 2, 0)
             transpose_h(r - 2, 1)
-            inverse_root(r)
             if ahead:
-                open_statistics(r + 1)
-                regroup_x(r + 1)
-                mean_square_on_vector(r + 1, range(on_vector))
-                quantise_x(r + 1)
-                mean_square_on_scalar(r + 1, range(on_vector, HALF))
+                transpose_x(r + 1)
+            inverse_root(r)
             regroup_h(r - 2, 0)
             regroup_h(r - 2, 1)
+
             quantise_h(r - 2, 0)
             quantise_h(r - 2, 1)
             for n in range(G_BANKS):
                 gate_matmul(r, n)
             for n in range(OUT_BANKS):
                 out_matmul(r - 2, n)
+            if ahead:
+                open_statistics(r + 1)
+                regroup_x(r + 1)
+                mean_square_on_vector(r + 1, range(on_vector))
+                quantise_x(r + 1)
             gate_times_norm(r - 1, range(HEADS))
             if ahead:
-                mean_square_on_scalar(r + 1, range(HALF, HEADS))
+                mean_square_on_scalar(r + 1, range(on_vector, HEADS))
             for n in range(OUT_BANKS):
                 store_out(r - 2, n)
         for half in range(2):

@@ -85,24 +85,30 @@ def tile_retnet_pc_kernel(tc, x, wg_words, wg_scales, ret, wo_words, wo_scales, 
         make_identity(nc, ident[:])
         warm = keep.tile([P, 1], F32)
         nc.scalar.activation(out=warm[:], in_=minus_half[:, 0:1], func=ACT.Silu)
-        load_planes(wg_planes, wg_scales, X_PASSES)
-        load_x(1)
-        load_ret(0)
-        for n in range(G_BANKS):
+        def load_wg(n):
             for g in range(X_PASSES):
                 nc.sync.dma_start(
                     out=wg_codes[:, g, N_TILE * n : N_TILE * (n + 1)].bitcast(I32),
                     in_=wg_words[g].rearrange("p n t -> p (n t)")[:, 4 * N_TILE * n : 4 * N_TILE * (n + 1)].bitcast(I32),
                 )
+
+        def load_wo():
+            for g in range(H_PASSES):
+                nc.sync.dma_start(
+                    out=wo_codes[:, g, :].bitcast(I32), in_=wo_words[g].rearrange("p n t -> p (n t)").bitcast(I32)
+                )
+
+        load_planes(wg_planes, wg_scales, X_PASSES)
+        load_planes(wo_planes, wo_scales, H_PASSES)
+        load_x(1)
+        load_ret(0)
+        for n in range(G_BANKS):
+            load_wg(n)
         load_x(2)
         load_x(3)
         load_ret(1)
         load_ret(2)
-        load_planes(wo_planes, wo_scales, H_PASSES)
-        for g in range(H_PASSES):
-            nc.sync.dma_start(
-                out=wo_codes[:, g, :].bitcast(I32), in_=wo_words[g].rearrange("p n t -> p (n t)").bitcast(I32)
-            )
+        load_wo()
         load_ret(3)
         for i in range(4, S_TILES):
             load_x(i)
@@ -121,8 +127,8 @@ def tile_retnet_pc_kernel(tc, x, wg_words, wg_scales, ret, wo_words, wo_scales, 
             regroup_two_passes(nc.vector.tensor_copy, x_grouped[i][:], x_bank[i])
 
         def quantise_x(i):
-            x_codes[i] = work.tile([P, X_PASSES, P], U32, tag="x_codes", align_bytes=64, name="x_codes")
-            x_scales[i] = work.tile([P, X_PASSES, P], U8, tag="x_scales", align_bytes=64, name="x_scales")
+            x_codes[i] = work.tile([P, X_PASSES, P], U32, tag="x_codes", bufs=4, align_bytes=64, name="x_codes")
+            x_scales[i] = work.tile([P, X_PASSES, P], U8, tag="x_scales", bufs=4, align_bytes=64, name="x_scales")
             quantise_two_passes(nc, x_codes[i][:], x_scales[i][:], x_grouped[i][:])
 
         def open_statistics(i):
@@ -175,7 +181,7 @@ def tile_retnet_pc_kernel(tc, x, wg_words, wg_scales, ret, wo_words, wo_scales, 
                     stop=(g == X_PASSES - 1),
                 )
             if n == 0:
-                silu[i] = work.tile([P, V], F32, tag="silu", name="silu")
+                silu[i] = work.tile([P, V], F32, tag="silu", bufs=4, name="silu")
             nc.scalar.activation(out=silu[i][:, cols], in_=acc[:], func=ACT.Silu)
 
         def gate_times_norm(i, heads):
@@ -232,7 +238,7 @@ def tile_retnet_pc_kernel(tc, x, wg_words, wg_scales, ret, wo_words, wo_scales, 
             copy(out=result[:], in_=out_banks[i, n][:])
             nc.sync.dma_start(out=out_rows[P * i : P * (i + 1), N_TILE * n : N_TILE * (n + 1)], in_=result[:])
 
-        on_vector = 1
+        on_vector = 0
         last = S_TILES - 1
         transpose_x(0)
         regroup_x(0)
@@ -241,49 +247,57 @@ def tile_retnet_pc_kernel(tc, x, wg_words, wg_scales, ret, wo_words, wo_scales, 
         open_statistics(0)
         mean_square_on_scalar(0, range(HALF))
         regroup_x(1)
-        mean_square_on_vector(0, range(HALF, HEADS))
-        inverse_root(0, 0, HALF)
+        mean_square_on_vector(0, (4,))
         quantise_x(1)
+        mean_square_on_vector(0, (5,))
+        inverse_root(0, 0, HALF)
+        mean_square_on_vector(0, (6, 7))
         inverse_root(0, HALF, HALF)
         for n in range(G_BANKS):
-            if n == G_BANKS - 1:
-                transpose_x(2)
             gate_matmul(0, n)
             gate_matmul(1, n)
-            gate_times_norm(0, (2 * n,))
-            if n == G_BANKS - 1:
-                regroup_x(2)
-            gate_times_norm(0, (2 * n + 1,))
+            if n < G_BANKS - 1:
+                gate_times_norm(0, (2 * n, 2 * n + 1))
+        transpose_x(2)
+        gate_times_norm(0, (6,))
+        regroup_x(2)
+        gate_times_norm(0, (7,))
         quantise_x(2)
         open_statistics(1)
-        mean_square_on_scalar(1, range(HALF))
-        mean_square_on_vector(1, range(HALF, HEADS))
+        mean_square_on_scalar(1, range(4, HEADS))
+        mean_square_on_vector(1, range(4))
         inverse_root(1)
         open_statistics(2)
-        mean_square_on_scalar(2, range(on_vector, HEADS))
-        mean_square_on_vector(2, range(on_vector))
         for r in range(2, S_TILES):
             ahead = r + 1 < S_TILES
             transpose_h(r - 2, 0)
             transpose_h(r - 2, 1)
             if ahead:
                 transpose_x(r + 1)
-            inverse_root(r)
+            if r > 2:
+                inverse_root(r)
             regroup_h(r - 2, 0)
             regroup_h(r - 2, 1)
-
+            if ahead:
+                regroup_x(r + 1)
             quantise_h(r - 2, 0)
             quantise_h(r - 2, 1)
+            if r == 2:
+                mean_square_on_vector(2, range(1))
             for n in range(G_BANKS):
                 gate_matmul(r, n)
+            if r == 2:
+                mean_square_on_scalar(2, range(1, HEADS))
             for n in range(OUT_BANKS):
                 out_matmul(r - 2, n)
             if ahead:
                 open_statistics(r + 1)
-                regroup_x(r + 1)
-                mean_square_on_vector(r + 1, range(on_vector))
                 quantise_x(r + 1)
+                mean_square_on_vector(r + 1, range(on_vector))
+
             gate_times_norm(r - 1, range(HEADS))
+            if r == 2:
+                inverse_root(2)
             if ahead:
                 mean_square_on_scalar(r + 1, range(on_vector, HEADS))
             for n in range(OUT_BANKS):

@@ -79,18 +79,18 @@ def tile_retnet_pc_kernel(tc, x, wg_words, wg_scales, ret, wo_words, wo_scales, 
         load_x(0)
         nc.vector.memset(wg_planes[:].bitcast(I32), 0)
         nc.vector.memset(wo_planes[:].bitcast(I32), 0)
-        minus_half = keep.tile([P, HEADS], F32)
+        minus_half = keep.tile([P, 2 * HEADS], F32)
         nc.vector.memset(minus_half[:], -0.5)
         ident = keep.tile([P, P], F32)
         make_identity(nc, ident[:])
         warm = keep.tile([P, 1], F32)
         nc.scalar.activation(out=warm[:], in_=minus_half[:, 0:1], func=ACT.Silu)
         def load_wg(n):
-            for g in range(X_PASSES):
-                nc.sync.dma_start(
-                    out=wg_codes[:, g, N_TILE * n : N_TILE * (n + 1)].bitcast(I32),
-                    in_=wg_words[g].rearrange("p n t -> p (n t)")[:, 4 * N_TILE * n : 4 * N_TILE * (n + 1)].bitcast(I32),
-                )
+            cols = slice(N_TILE * n, N_TILE * (n + 1))
+            nc.sync.dma_start(
+                out=wg_codes[:, :, cols].bitcast(I32),
+                in_=wg_words.bitcast(I32).rearrange("g p n t -> p g (n t)")[:, :, cols],
+            )
 
         def load_wo():
             for g in range(H_PASSES):
@@ -99,7 +99,6 @@ def tile_retnet_pc_kernel(tc, x, wg_words, wg_scales, ret, wo_words, wo_scales, 
                 )
 
         load_planes(wg_planes, wg_scales, X_PASSES)
-        load_planes(wo_planes, wo_scales, H_PASSES)
         load_x(1)
         load_ret(0)
         for n in range(G_BANKS):
@@ -108,6 +107,7 @@ def tile_retnet_pc_kernel(tc, x, wg_words, wg_scales, ret, wo_words, wo_scales, 
         load_x(3)
         load_ret(1)
         load_ret(2)
+        load_planes(wo_planes, wo_scales, H_PASSES)
         load_wo()
         load_ret(3)
         for i in range(4, S_TILES):
@@ -115,7 +115,7 @@ def tile_retnet_pc_kernel(tc, x, wg_words, wg_scales, ret, wo_words, wo_scales, 
             load_ret(i)
 
         x_bank, x_grouped, x_codes, x_scales = {}, {}, {}, {}
-        mean_sq, rstd, silu, h_sb = {}, {}, {}, {}
+        silu, h_sb = {}, {}
         h_banks, h_grouped, h_codes, h_scales, out_banks = {}, {}, {}, {}, {}
 
         def transpose_x(i):
@@ -131,41 +131,42 @@ def tile_retnet_pc_kernel(tc, x, wg_words, wg_scales, ret, wo_words, wo_scales, 
             x_scales[i] = work.tile([P, X_PASSES, P], U8, tag="x_scales", bufs=4, align_bytes=64, name="x_scales")
             quantise_two_passes(nc, x_codes[i][:], x_scales[i][:], x_grouped[i][:])
 
-        def open_statistics(i):
-            mean_sq[i] = work.tile([P, HEADS], F32, tag="mean_sq", name="mean_sq")
+        mean_sq = keep.tile([P, HEADS * S_TILES], F32)
+        rstd = keep.tile([P, HEADS * S_TILES], F32)
 
-        def mean_square_on_scalar(i, heads):
-            for head in heads:
+        def head_of_ret(column):
+            head = column % HEADS
+            return ret_sb[column // HEADS][:, HEAD_DIM * head : HEAD_DIM * (head + 1)]
+
+        def mean_square_on_scalar(columns):
+            for column in columns:
                 squares = work.tile([P, HEAD_DIM], BF16, tag="squares")
                 nc.scalar.activation(
                     out=squares[:],
-                    in_=ret_sb[i][:, HEAD_DIM * head : HEAD_DIM * (head + 1)],
+                    in_=head_of_ret(column),
                     func=ACT.Square,
                     scale=HEAD_DIM ** -0.5,
-                    accum_out=mean_sq[i][:, head : head + 1],
+                    accum_out=mean_sq[:, column : column + 1],
                 )
 
-        def mean_square_on_vector(i, heads):
-            for head in heads:
+        def mean_square_on_vector(columns):
+            for column in columns:
                 squares = work.tile([P, HEAD_DIM], BF16, tag="squares_v")
-                cols = slice(HEAD_DIM * head, HEAD_DIM * (head + 1))
                 nc.vector.scalar_tensor_tensor(
                     out=squares[:],
-                    in0=ret_sb[i][:, cols],
+                    in0=head_of_ret(column),
                     scalar=1.0 / HEAD_DIM,
-                    in1=ret_sb[i][:, cols],
+                    in1=head_of_ret(column),
                     op0=ALU.mult,
                     op1=ALU.mult,
-                    accum_out=mean_sq[i][:, head : head + 1],
+                    accum_out=mean_sq[:, column : column + 1],
                 )
 
-        def inverse_root(i, first=0, count=HEADS):
-            cols = slice(first, first + count)
-            shifted = work.tile([P, HEADS], F32, tag="shifted")
-            nc.vector.tensor_scalar(out=shifted[:, cols], in0=mean_sq[i][:, cols], scalar1=EPS, scalar2=None, op0=ALU.add)
-            if i not in rstd:
-                rstd[i] = work.tile([P, HEADS], F32, tag="rstd", name="rstd")
-            nc.gpsimd.tensor_tensor(out=rstd[i][:, cols], in0=shifted[:, cols], in1=minus_half[:, cols], op=ALU.pow)
+        def inverse_root(first, end):
+            cols = slice(first, end)
+            shifted = work.tile([P, end - first], F32, tag="shifted")
+            nc.vector.tensor_scalar(out=shifted[:], in0=mean_sq[:, cols], scalar1=EPS, scalar2=None, op0=ALU.add)
+            nc.gpsimd.tensor_tensor(out=rstd[:, cols], in0=shifted[:], in1=minus_half[:, : end - first], op=ALU.pow)
 
         def gate_matmul(i, n):
             cols = slice(N_TILE * n, N_TILE * (n + 1))
@@ -196,7 +197,7 @@ def tile_retnet_pc_kernel(tc, x, wg_words, wg_scales, ret, wo_words, wo_scales, 
                     nc.vector.scalar_tensor_tensor(
                         out=h_sb[i][:, start : start + P].rearrange("s (p e) -> s p e", e=2),
                         in0=silu_words[:, u],
-                        scalar=rstd[i][:, head : head + 1],
+                        scalar=rstd[:, HEADS * i + head : HEADS * i + head + 1],
                         in1=ret_words[:, u],
                         op0=ALU.mult,
                         op1=ALU.mult,
@@ -238,21 +239,23 @@ def tile_retnet_pc_kernel(tc, x, wg_words, wg_scales, ret, wo_words, wo_scales, 
             copy(out=result[:], in_=out_banks[i, n][:])
             nc.sync.dma_start(out=out_rows[P * i : P * (i + 1), N_TILE * n : N_TILE * (n + 1)], in_=result[:])
 
-        on_vector = 0
         last = S_TILES - 1
+
+        def ready_columns(r):
+            return HEADS + HEADS * last * (r - 1) // (last - 1)
+
         transpose_x(0)
         regroup_x(0)
         transpose_x(1)
         quantise_x(0)
-        open_statistics(0)
-        mean_square_on_scalar(0, range(HALF))
+        mean_square_on_scalar(range(HALF))
         regroup_x(1)
-        mean_square_on_vector(0, (4,))
+        mean_square_on_vector((4,))
         quantise_x(1)
-        mean_square_on_vector(0, (5,))
-        inverse_root(0, 0, HALF)
-        mean_square_on_vector(0, (6, 7))
-        inverse_root(0, HALF, HALF)
+        mean_square_on_vector((5,))
+        inverse_root(0, HALF)
+        mean_square_on_vector((6, 7))
+        inverse_root(HALF, HEADS)
         for n in range(G_BANKS):
             gate_matmul(0, n)
             gate_matmul(1, n)
@@ -263,45 +266,34 @@ def tile_retnet_pc_kernel(tc, x, wg_words, wg_scales, ret, wo_words, wo_scales, 
         regroup_x(2)
         gate_times_norm(0, (7,))
         quantise_x(2)
-        open_statistics(1)
-        mean_square_on_scalar(1, range(4, HEADS))
-        mean_square_on_vector(1, range(4))
-        inverse_root(1)
-        open_statistics(2)
+        mean_square_on_scalar(range(HEADS + 2, ready_columns(2)))
+        mean_square_on_vector(range(HEADS, HEADS + 2))
         for r in range(2, S_TILES):
             ahead = r + 1 < S_TILES
             transpose_h(r - 2, 0)
             transpose_h(r - 2, 1)
             if ahead:
                 transpose_x(r + 1)
-            if r > 2:
-                inverse_root(r)
+            inverse_root(ready_columns(r - 1), ready_columns(r))
+
             regroup_h(r - 2, 0)
             regroup_h(r - 2, 1)
             if ahead:
                 regroup_x(r + 1)
             quantise_h(r - 2, 0)
             quantise_h(r - 2, 1)
-            if r == 2:
-                mean_square_on_vector(2, range(1))
             for n in range(G_BANKS):
                 gate_matmul(r, n)
-            if r == 2:
-                mean_square_on_scalar(2, range(1, HEADS))
             for n in range(OUT_BANKS):
                 out_matmul(r - 2, n)
             if ahead:
-                open_statistics(r + 1)
                 quantise_x(r + 1)
-                mean_square_on_vector(r + 1, range(on_vector))
-
             gate_times_norm(r - 1, range(HEADS))
-            if r == 2:
-                inverse_root(2)
             if ahead:
-                mean_square_on_scalar(r + 1, range(on_vector, HEADS))
-            for n in range(OUT_BANKS):
-                store_out(r - 2, n)
+                mean_square_on_vector(range(ready_columns(r), ready_columns(r) + 1))
+                mean_square_on_scalar(range(ready_columns(r) + 1, ready_columns(r + 1)))
+            store_out(r - 2, 0)
+            store_out(r - 2, 1)
         for half in range(2):
             transpose_h(last - 1, half)
             regroup_h(last - 1, half, nc.scalar.copy)

@@ -81,16 +81,18 @@ def tile_retnet_pc_kernel(tc, x, wg_words, wg_scales, ret, wo_words, wo_scales, 
         nc.vector.memset(wo_planes[:].bitcast(I32), 0)
         minus_half = keep.tile([P, 2 * HEADS], F32)
         nc.vector.memset(minus_half[:], -0.5)
+        ones = keep.tile([P, N_TILE], BF16)
+        nc.gpsimd.memset(ones[:], 1.0)
         ident = keep.tile([P, P], F32)
         make_identity(nc, ident[:])
         warm = keep.tile([P, 1], F32)
         nc.scalar.activation(out=warm[:], in_=minus_half[:, 0:1], func=ACT.Silu)
         def load_wg(n):
-            cols = slice(N_TILE * n, N_TILE * (n + 1))
-            nc.sync.dma_start(
-                out=wg_codes[:, :, cols].bitcast(I32),
-                in_=wg_words.bitcast(I32).rearrange("g p n t -> p g (n t)")[:, :, cols],
-            )
+            for g in range(X_PASSES):
+                nc.sync.dma_start(
+                    out=wg_codes[:, g, N_TILE * n : N_TILE * (n + 1)].bitcast(I32),
+                    in_=wg_words[g].rearrange("p n t -> p (n t)")[:, 4 * N_TILE * n : 4 * N_TILE * (n + 1)].bitcast(I32),
+                )
 
         def load_wo():
             for g in range(H_PASSES):
@@ -117,6 +119,11 @@ def tile_retnet_pc_kernel(tc, x, wg_words, wg_scales, ret, wo_words, wo_scales, 
         x_bank, x_grouped, x_codes, x_scales = {}, {}, {}, {}
         silu, h_sb = {}, {}
         h_banks, h_grouped, h_codes, h_scales, out_banks = {}, {}, {}, {}, {}
+
+        def keep_tensor_busy(count, tag, bufs):
+            unread = psum.tile([P, N_TILE], F32, tag=tag, bufs=bufs, name="unread")
+            for turn in range(count):
+                nc.tensor.matmul(unread[:], lhsT=ones[:, :P], rhs=ones[:], start=True, stop=True)
 
         def transpose_x(i):
             x_bank[i] = psum.tile([P, 2, 2, P], F32, tag="xt", name="xt")
@@ -244,8 +251,10 @@ def tile_retnet_pc_kernel(tc, x, wg_words, wg_scales, ret, wo_words, wo_scales, 
         def ready_columns(r):
             return HEADS + HEADS * last * (r - 1) // (last - 1)
 
+        keep_tensor_busy(4, "o", 2)
         transpose_x(0)
         regroup_x(0)
+        keep_tensor_busy(2, "o", 2)
         transpose_x(1)
         quantise_x(0)
         mean_square_on_scalar(range(HALF))
@@ -256,12 +265,14 @@ def tile_retnet_pc_kernel(tc, x, wg_words, wg_scales, ret, wo_words, wo_scales, 
         inverse_root(0, HALF)
         mean_square_on_vector((6, 7))
         inverse_root(HALF, HEADS)
+        keep_tensor_busy(2, "o", 2)
         for n in range(G_BANKS):
             gate_matmul(0, n)
             gate_matmul(1, n)
             if n < G_BANKS - 1:
                 gate_times_norm(0, (2 * n, 2 * n + 1))
         transpose_x(2)
+        keep_tensor_busy(2, "o", 2)
         gate_times_norm(0, (6,))
         regroup_x(2)
         gate_times_norm(0, (7,))
@@ -290,8 +301,8 @@ def tile_retnet_pc_kernel(tc, x, wg_words, wg_scales, ret, wo_words, wo_scales, 
                 quantise_x(r + 1)
             gate_times_norm(r - 1, range(HEADS))
             if ahead:
-                mean_square_on_vector(range(ready_columns(r), ready_columns(r) + 1))
-                mean_square_on_scalar(range(ready_columns(r) + 1, ready_columns(r + 1)))
+                mean_square_on_vector(range(ready_columns(r), ready_columns(r) + 2))
+                mean_square_on_scalar(range(ready_columns(r) + 2, ready_columns(r + 1)))
             store_out(r - 2, 0)
             store_out(r - 2, 1)
         for half in range(2):

@@ -88,11 +88,11 @@ def tile_retnet_pc_kernel(tc, x, wg_words, wg_scales, ret, wo_words, wo_scales, 
         warm = keep.tile([P, 1], F32)
         nc.scalar.activation(out=warm[:], in_=minus_half[:, 0:1], func=ACT.Silu)
         def load_wg(n):
-            for g in range(X_PASSES):
-                nc.sync.dma_start(
-                    out=wg_codes[:, g, N_TILE * n : N_TILE * (n + 1)].bitcast(I32),
-                    in_=wg_words[g].rearrange("p n t -> p (n t)")[:, 4 * N_TILE * n : 4 * N_TILE * (n + 1)].bitcast(I32),
-                )
+            cols = slice(N_TILE * n, N_TILE * (n + 1))
+            nc.sync.dma_start(
+                out=wg_codes[:, :, cols].bitcast(I32),
+                in_=wg_words.bitcast(I32).rearrange("g p n t -> p g (n t)")[:, :, cols],
+            )
 
         def load_wo():
             for g in range(H_PASSES):
@@ -301,8 +301,9 @@ def tile_retnet_pc_kernel(tc, x, wg_words, wg_scales, ret, wo_words, wo_scales, 
                 quantise_x(r + 1)
             gate_times_norm(r - 1, range(HEADS))
             if ahead:
-                mean_square_on_vector(range(ready_columns(r), ready_columns(r) + 2))
-                mean_square_on_scalar(range(ready_columns(r) + 2, ready_columns(r + 1)))
+                mean_square_on_scalar(range(ready_columns(r) + (2 if r > 2 else 0), ready_columns(r + 1)))
+            if r + 2 < S_TILES:
+                mean_square_on_vector(range(ready_columns(r + 1), ready_columns(r + 1) + 2))
             store_out(r - 2, 0)
             store_out(r - 2, 1)
         for half in range(2):

@@ -309,6 +309,7 @@ def tile_retnet_pc_kernel(tc, x, wg_words, wg_scales, ret, wo_words, wo_scales, 
         for half in range(2):
             transpose_h(last - 1, half)
             regroup_h(last - 1, half, nc.scalar.copy)
+        keep_tensor_busy(2, "g", 3)
         gate_times_norm(last, range(HALF))
         quantise_h(last - 1, 0)
         quantise_h(last - 1, 1)

@@ -56,10 +56,10 @@ def tile_retnet_pc_kernel(tc, x, wg_words, wg_scales, ret, wo_words, wo_scales, 
     with tc.tile_pool(name="keep", bufs=1) as keep, tc.tile_pool(name="work", bufs=3) as work, tc.psum_pool(
         name="psum", bufs=1
     ) as psum, tc.manual_schedule():
-        wg_planes = keep.tile([P, V], U8, align_bytes=64)
-        wo_planes = keep.tile([P, E], U8, align_bytes=64)
-        wg_codes = keep.tile([P, X_PASSES, V], U32, align_bytes=64)
-        wo_codes = keep.tile([P, H_PASSES, E], U32, align_bytes=64)
+        wg_planes = keep.tile([P, V], U8, align_bytes=256)
+        wo_planes = keep.tile([P, E], U8, align_bytes=256)
+        wg_codes = keep.tile([P, X_PASSES, V], U32, align_bytes=256)
+        wo_codes = keep.tile([P, H_PASSES, E], U32, align_bytes=256)
         x_sb = [keep.tile([P, E], BF16, name="x_sb%d" % i) for i in range(S_TILES)]
         ret_sb = [keep.tile([P, V], BF16, name="ret_sb%d" % i) for i in range(S_TILES)]
 
@@ -130,12 +130,12 @@ def tile_retnet_pc_kernel(tc, x, wg_words, wg_scales, ret, wo_words, wo_scales, 
             transpose_two_passes(nc, x_bank[i], x_sb[i][:].bitcast(F32), 0, ident, 2)
 
         def regroup_x(i):
-            x_grouped[i] = work.tile([P, X_PASSES, P, 4], BF16, tag="x_grouped", align_bytes=64, name="x_grouped")
+            x_grouped[i] = work.tile([P, X_PASSES, P, 4], BF16, tag="x_grouped", align_bytes=256, name="x_grouped")
             regroup_two_passes(nc.vector.tensor_copy, x_grouped[i][:], x_bank[i])
 
         def quantise_x(i):
-            x_codes[i] = work.tile([P, X_PASSES, P], U32, tag="x_codes", bufs=4, align_bytes=64, name="x_codes")
-            x_scales[i] = work.tile([P, X_PASSES, P], U8, tag="x_scales", bufs=4, align_bytes=64, name="x_scales")
+            x_codes[i] = work.tile([P, X_PASSES, P], U32, tag="x_codes", bufs=4, align_bytes=256, name="x_codes")
+            x_scales[i] = work.tile([P, X_PASSES, P], U8, tag="x_scales", bufs=4, align_bytes=256, name="x_scales")
             quantise_two_passes(nc, x_codes[i][:], x_scales[i][:], x_grouped[i][:])
 
         mean_sq = keep.tile([P, HEADS * S_TILES], F32)
@@ -216,13 +216,13 @@ def tile_retnet_pc_kernel(tc, x, wg_words, wg_scales, ret, wo_words, wo_scales, 
 
         def regroup_h(i, half, copy=nc.vector.tensor_copy):
             if i not in h_grouped:
-                h_grouped[i] = work.tile([P, H_PASSES, P, 4], BF16, tag="h_grouped", align_bytes=64, name="h_grouped")
+                h_grouped[i] = work.tile([P, H_PASSES, P, 4], BF16, tag="h_grouped", align_bytes=256, name="h_grouped")
             regroup_two_passes(copy, h_grouped[i][:, 2 * half : 2 * half + 2], h_banks[i, half])
 
         def quantise_h(i, half):
             if i not in h_codes:
-                h_codes[i] = work.tile([P, H_PASSES, P], U32, tag="h_codes", bufs=4, align_bytes=64, name="h_codes")
-                h_scales[i] = work.tile([P, H_PASSES, P], U8, tag="h_scales", bufs=4, align_bytes=64, name="h_scales")
+                h_codes[i] = work.tile([P, H_PASSES, P], U32, tag="h_codes", bufs=4, align_bytes=256, name="h_codes")
+                h_scales[i] = work.tile([P, H_PASSES, P], U8, tag="h_scales", bufs=4, align_bytes=256, name="h_scales")
             two = slice(2 * half, 2 * half + 2)
             quantise_two_passes(nc, h_codes[i][:, two], h_scales[i][:, two], h_grouped[i][:, two])
 

@@ -103,8 +103,10 @@ def tile_retnet_pc_kernel(tc, x, wg_words, wg_scales, ret, wo_words, wo_scales, 
         load_planes(wg_planes, wg_scales, X_PASSES)
         load_x(1)
         load_ret(0)
-        for n in range(G_BANKS):
-            load_wg(n)
+        load_wg(0)
+        load_wg(1)
+        load_wg(2)
+        load_wg(3)
         load_x(2)
         load_x(3)
         load_ret(1)
@@ -112,10 +114,14 @@ def tile_retnet_pc_kernel(tc, x, wg_words, wg_scales, ret, wo_words, wo_scales, 
         load_planes(wo_planes, wo_scales, H_PASSES)
         load_wo()
         load_ret(3)
-        for i in range(4, S_TILES):
-            load_x(i)
-            load_ret(i)
-
+        load_x(4)
+        load_ret(4)
+        load_x(5)
+        load_ret(5)
+        load_x(6)
+        load_ret(6)
+        load_x(7)
+        load_ret(7)
         x_bank, x_grouped, x_codes, x_scales = {}, {}, {}, {}
         silu, h_sb = {}, {}
         h_banks, h_grouped, h_codes, h_scales, out_banks = {}, {}, {}, {}, {}
@@ -134,8 +140,8 @@ def tile_retnet_pc_kernel(tc, x, wg_words, wg_scales, ret, wo_words, wo_scales, 
             regroup_two_passes(nc.vector.tensor_copy, x_grouped[i][:], x_bank[i])
 
         def quantise_x(i):
-            x_codes[i] = work.tile([P, X_PASSES, P], U32, tag="x_codes", bufs=4, align_bytes=256, name="x_codes")
-            x_scales[i] = work.tile([P, X_PASSES, P], U8, tag="x_scales", bufs=4, align_bytes=256, name="x_scales")
+            x_codes[i] = work.tile([P, X_PASSES, P], U32, tag="x_codes", bufs=5, align_bytes=256, name="x_codes")
+            x_scales[i] = work.tile([P, X_PASSES, P], U8, tag="x_scales", bufs=5, align_bytes=256, name="x_scales")
             quantise_two_passes(nc, x_codes[i][:], x_scales[i][:], x_grouped[i][:])
 
         mean_sq = keep.tile([P, HEADS * S_TILES], F32)
@@ -189,7 +195,7 @@ def tile_retnet_pc_kernel(tc, x, wg_words, wg_scales, ret, wo_words, wo_scales, 
                     stop=(g == X_PASSES - 1),
                 )
             if n == 0:
-                silu[i] = work.tile([P, V], F32, tag="silu", bufs=4, name="silu")
+                silu[i] = work.tile([P, V], F32, tag="silu", bufs=5, name="silu")
             nc.scalar.activation(out=silu[i][:, cols], in_=acc[:], func=ACT.Silu)
 
         def gate_times_norm(i, heads):
@@ -286,13 +292,16 @@ def tile_retnet_pc_kernel(tc, x, wg_words, wg_scales, ret, wo_words, wo_scales, 
             if ahead:
                 transpose_x(r + 1)
             inverse_root(ready_columns(r - 1), ready_columns(r))
-
             regroup_h(r - 2, 0)
             regroup_h(r - 2, 1)
             if ahead:
                 regroup_x(r + 1)
             quantise_h(r - 2, 0)
             quantise_h(r - 2, 1)
+            first, end = (ready_columns(r), ready_columns(r + 1)) if ahead else (0, 0)
+            on_vector = (2 if r < 4 else 1) if ahead else 0
+            squares = list(range(first + on_vector, end))
+            mean_square_on_scalar(squares[:3])
             for n in range(G_BANKS):
                 gate_matmul(r, n)
             for n in range(OUT_BANKS):
@@ -300,10 +309,8 @@ def tile_retnet_pc_kernel(tc, x, wg_words, wg_scales, ret, wo_words, wo_scales, 
             if ahead:
                 quantise_x(r + 1)
             gate_times_norm(r - 1, range(HEADS))
-            if ahead:
-                mean_square_on_scalar(range(ready_columns(r) + (2 if r > 2 else 0), ready_columns(r + 1)))
-            if r + 2 < S_TILES:
-                mean_square_on_vector(range(ready_columns(r + 1), ready_columns(r + 1) + 2))
+            mean_square_on_scalar(squares[3:])
+            mean_square_on_vector(range(first, first + on_vector))
             store_out(r - 2, 0)
             store_out(r - 2, 1)
         for half in range(2):

@@ -232,13 +232,13 @@ def tile_retnet_pc_kernel(tc, x, wg_words, wg_scales, ret, wo_words, wo_scales, 
             two = slice(2 * half, 2 * half + 2)
             quantise_two_passes(nc, h_codes[i][:, two], h_scales[i][:, two], h_grouped[i][:, two])
 
-        def out_matmul(i, n, passes=range(H_PASSES)):
-            cols = slice(N_TILE * n, N_TILE * (n + 1))
-            if (i, n) not in out_banks:
-                out_banks[i, n] = psum.tile([P, N_TILE], F32, tag="o", bufs=2, name="o")
+        def out_matmul(i, n, passes=range(H_PASSES), tag="o", bufs=2, width=N_TILE):
+            cols = slice(width * n, width * (n + 1))
+            if (i, n, width) not in out_banks:
+                out_banks[i, n, width] = psum.tile([P, N_TILE], F32, tag=tag, bufs=bufs, name="o")
             for g in passes:
                 nc.tensor.matmul_mx(
-                    out=out_banks[i, n][:],
+                    out=out_banks[i, n, width][:, :width],
                     lhsT=h_codes[i][:, g, :].bitcast(FP8X4),
                     lhsT_scale=h_scales[i][:, g, :],
                     rhs=wo_codes[:, g, cols].bitcast(FP8X4),
@@ -247,10 +247,10 @@ def tile_retnet_pc_kernel(tc, x, wg_words, wg_scales, ret, wo_words, wo_scales, 
                     stop=(g == H_PASSES - 1),
                 )
 
-        def store_out(i, n, copy=nc.scalar.copy):
-            result = work.tile([P, N_TILE], F32, tag="result", bufs=4)
-            copy(out=result[:], in_=out_banks[i, n][:])
-            nc.sync.dma_start(out=out_rows[P * i : P * (i + 1), N_TILE * n : N_TILE * (n + 1)], in_=result[:])
+        def store_out(i, n, copy=nc.scalar.copy, width=N_TILE):
+            result = work.tile([P, N_TILE], F32, tag="result", bufs=8)
+            copy(out=result[:, :width], in_=out_banks[i, n, width][:, :width])
+            nc.sync.dma_start(out=out_rows[P * i : P * (i + 1), width * n : width * (n + 1)], in_=result[:, :width])
 
         last = S_TILES - 1
 
@@ -285,54 +285,66 @@ def tile_retnet_pc_kernel(tc, x, wg_words, wg_scales, ret, wo_words, wo_scales, 
         quantise_x(2)
         mean_square_on_scalar(range(HEADS + 2, ready_columns(2)))
         mean_square_on_vector(range(HEADS, HEADS + 2))
-        for r in range(2, S_TILES):
-            ahead = r + 1 < S_TILES
+        for r in range(2, last):
             transpose_h(r - 2, 0)
             transpose_h(r - 2, 1)
-            if ahead:
-                transpose_x(r + 1)
+            transpose_x(r + 1)
             inverse_root(ready_columns(r - 1), ready_columns(r))
             regroup_h(r - 2, 0)
             regroup_h(r - 2, 1)
-            if ahead:
-                regroup_x(r + 1)
+            regroup_x(r + 1)
             quantise_h(r - 2, 0)
             quantise_h(r - 2, 1)
-            first, end = (ready_columns(r), ready_columns(r + 1)) if ahead else (0, 0)
-            on_vector = (2 if r < 4 else 1) if ahead else 0
+            first, end = ready_columns(r), ready_columns(r + 1)
+            on_vector = 2 if r < 4 else 1
             squares = list(range(first + on_vector, end))
             mean_square_on_scalar(squares[:3])
             for n in range(G_BANKS):
                 gate_matmul(r, n)
             for n in range(OUT_BANKS):
                 out_matmul(r - 2, n)
-            if ahead:
-                quantise_x(r + 1)
-            gate_times_norm(r - 1, range(HEADS))
-            mean_square_on_scalar(squares[3:])
+            quantise_x(r + 1)
+            gate_times_norm(r - 1, range(6))
             mean_square_on_vector(range(first, first + on_vector))
+            gate_times_norm(r - 1, range(6, HEADS))
+            mean_square_on_scalar(squares[3:])
             store_out(r - 2, 0)
             store_out(r - 2, 1)
-        for half in range(2):
-            transpose_h(last - 1, half)
-            regroup_h(last - 1, half, nc.scalar.copy)
-        keep_tensor_busy(2, "g", 3)
+        transpose_h(last - 2, 0)
+        transpose_h(last - 2, 1)
+        inverse_root(ready_columns(last - 1), ready_columns(last))
+        regroup_h(last - 2, 0)
+        regroup_h(last - 2, 1)
+        quantise_h(last - 2, 0)
+        quantise_h(last - 2, 1)
+        for n in range(G_BANKS):
+            gate_matmul(last, n)
+        gate_times_norm(last - 1, range(HEADS))
+        out_matmul(last - 2, 0)
+        transpose_h(last - 1, 0)
+        transpose_h(last - 1, 1)
+        regroup_h(last - 1, 0, nc.scalar.copy)
+        regroup_h(last - 1, 1, nc.scalar.copy)
+        out_matmul(last - 2, 1)
         gate_times_norm(last, range(HALF))
         quantise_h(last - 1, 0)
         quantise_h(last - 1, 1)
+        store_out(last - 2, 0)
         gate_times_norm(last, range(HALF, HEADS))
+        out_matmul(last - 1, 0)
+        store_out(last - 2, 1)
         transpose_h(last, 0)
-        regroup_h(last, 0, nc.scalar.copy)
-        for n in range(OUT_BANKS):
-            out_matmul(last - 1, n)
-        quantise_h(last, 0)
         transpose_h(last, 1)
+        regroup_h(last, 0, nc.scalar.copy)
         regroup_h(last, 1)
+        out_matmul(last - 1, 1)
+        store_out(last - 1, 0)
+        quantise_h(last, 0)
         quantise_h(last, 1)
-        for n in range(OUT_BANKS):
-            store_out(last - 1, n)
-        for passes in (range(0, 2), range(2, H_PASSES)):
-            for n in range(OUT_BANKS):
-                out_matmul(last, n, passes)
-        store_out(last, 0)
-        store_out(last, 1, nc.vector.tensor_copy)
+        store_out(last - 1, 1)
+        half_bank = N_TILE // 2
+        for n in range(4):
+            out_matmul(last, n, range(0, 2), tag=("g", "o")[n // 3], bufs=3 - n // 3, width=half_bank)
+        for n in range(4):
+            out_matmul(last, n, range(2, H_PASSES), width=half_bank)
+            store_out(last, n, (nc.scalar.copy, nc.vector.tensor_copy)[n % 2], half_bank)

@@ -285,34 +285,35 @@ def tile_retnet_pc_kernel(tc, x, wg_words, wg_scales, ret, wo_words, wo_scales, 
         quantise_x(2)
         mean_square_on_scalar(range(HEADS + 2, ready_columns(2)))
         mean_square_on_vector(range(HEADS, HEADS + 2))
+        inverse_root(HEADS, ready_columns(2))
         for r in range(2, last):
             transpose_h(r - 2, 0)
             transpose_h(r - 2, 1)
+            if r == 2:
+                keep_tensor_busy(2, "o", 2)
             transpose_x(r + 1)
-            inverse_root(ready_columns(r - 1), ready_columns(r))
             regroup_h(r - 2, 0)
             regroup_h(r - 2, 1)
-            regroup_x(r + 1)
             quantise_h(r - 2, 0)
             quantise_h(r - 2, 1)
             first, end = ready_columns(r), ready_columns(r + 1)
             on_vector = 2 if r < 4 else 1
+            mean_square_on_vector(range(first, first + on_vector))
             squares = list(range(first + on_vector, end))
-            mean_square_on_scalar(squares[:3])
+            mean_square_on_scalar(squares[:4])
             for n in range(G_BANKS):
                 gate_matmul(r, n)
+            gate_times_norm(r - 1, range(HEADS))
             for n in range(OUT_BANKS):
                 out_matmul(r - 2, n)
+            mean_square_on_scalar(squares[4:])
+            regroup_x(r + 1)
+            inverse_root(first, end)
             quantise_x(r + 1)
-            gate_times_norm(r - 1, range(6))
-            mean_square_on_vector(range(first, first + on_vector))
-            gate_times_norm(r - 1, range(6, HEADS))
-            mean_square_on_scalar(squares[3:])
             store_out(r - 2, 0)
             store_out(r - 2, 1)
         transpose_h(last - 2, 0)
         transpose_h(last - 2, 1)
-        inverse_root(ready_columns(last - 1), ready_columns(last))
         regroup_h(last - 2, 0)
         regroup_h(last - 2, 1)
         quantise_h(last - 2, 0)

@@ -255,7 +255,7 @@ def tile_retnet_pc_kernel(tc, x, wg_words, wg_scales, ret, wo_words, wo_scales, 
         last = S_TILES - 1
 
         def ready_columns(r):
-            return HEADS + HEADS * last * (r - 1) // (last - 1)
+            return [0,8,17,26,36,45,54,64][r]
 
         keep_tensor_busy(4, "o", 2)
         transpose_x(0)
@@ -287,29 +287,39 @@ def tile_retnet_pc_kernel(tc, x, wg_words, wg_scales, ret, wo_words, wo_scales, 
         mean_square_on_vector(range(HEADS, HEADS + 2))
         inverse_root(HEADS, ready_columns(2))
         for r in range(2, last):
+            early = 1 if r == 3 else 0
+            for n in range(early):
+                gate_matmul(r, n)
             transpose_h(r - 2, 0)
             transpose_h(r - 2, 1)
-            if r == 2:
-                keep_tensor_busy(2, "o", 2)
             transpose_x(r + 1)
             regroup_h(r - 2, 0)
             regroup_h(r - 2, 1)
+            if r == 2:
+                regroup_x(3)
             quantise_h(r - 2, 0)
             quantise_h(r - 2, 1)
+            if r == 2:
+                quantise_x(3)
             first, end = ready_columns(r), ready_columns(r + 1)
-            on_vector = 2 if r < 4 else 1
+            on_vector = [1,1,1,1,1][r - 2]
             mean_square_on_vector(range(first, first + on_vector))
             squares = list(range(first + on_vector, end))
-            mean_square_on_scalar(squares[:4])
-            for n in range(G_BANKS):
+            mean_square_on_scalar(squares[:[4,4,4,4,4][r - 2]])
+            for n in range(early, G_BANKS):
                 gate_matmul(r, n)
             gate_times_norm(r - 1, range(HEADS))
             for n in range(OUT_BANKS):
                 out_matmul(r - 2, n)
-            mean_square_on_scalar(squares[4:])
-            regroup_x(r + 1)
-            inverse_root(first, end)
-            quantise_x(r + 1)
+            mean_square_on_scalar(squares[[4,4,4,4,4][r - 2]:])
+            if r > 2:
+                regroup_x(r + 1)
+            if r + 1 < last:
+                inverse_root(first, end)
+            if r > 2:
+                quantise_x(r + 1)
+            if r + 1 == last:
+                inverse_root(first, end)
             store_out(r - 2, 0)
             store_out(r - 2, 1)
         transpose_h(last - 2, 0)
@@ -332,20 +342,20 @@ def tile_retnet_pc_kernel(tc, x, wg_words, wg_scales, ret, wo_words, wo_scales, 
         quantise_h(last - 1, 1)
         store_out(last - 2, 0)
         gate_times_norm(last, range(HALF, HEADS))
-        out_matmul(last - 1, 0)
+        out_matmul(last - 1, 0, tag="g", bufs=3)
         store_out(last - 2, 1)
         transpose_h(last, 0)
         transpose_h(last, 1)
         regroup_h(last, 0, nc.scalar.copy)
         regroup_h(last, 1)
-        out_matmul(last - 1, 1)
+        out_matmul(last - 1, 1, tag="g", bufs=3)
         store_out(last - 1, 0)
         quantise_h(last, 0)
         quantise_h(last, 1)
         store_out(last - 1, 1)
         half_bank = N_TILE // 2
         for n in range(4):
-            out_matmul(last, n, range(0, 2), tag=("g", "o")[n // 3], bufs=3 - n // 3, width=half_bank)
+            out_matmul(last, n, range(0, 2), tag=("o", "g")[n // 2], bufs=2 + n // 2, width=half_bank)
         for n in range(4):
             out_matmul(last, n, range(2, H_PASSES), width=half_bank)
             store_out(last, n, (nc.scalar.copy, nc.vector.tensor_copy)[n % 2], half_bank)

@@ -60,8 +60,10 @@ def tile_retnet_pc_kernel(tc, x, wg_words, wg_scales, ret, wo_words, wo_scales, 
         wo_planes = keep.tile([P, E], U8, align_bytes=256)
         wg_codes = keep.tile([P, X_PASSES, V], U32, align_bytes=256)
         wo_codes = keep.tile([P, H_PASSES, E], U32, align_bytes=256)
-        x_sb = [keep.tile([P, E], BF16, name="x_sb%d" % i) for i in range(S_TILES)]
-        ret_sb = [keep.tile([P, V], BF16, name="ret_sb%d" % i) for i in range(S_TILES)]
+        x_pairs = [keep.tile([P, 2, E], BF16, name="x_pair%d" % j) for j in range(S_TILES // 2)]
+        ret_pairs = [keep.tile([P, 2, V], BF16, name="ret_pair%d" % j) for j in range(S_TILES // 2)]
+        x_sb = [x_pairs[i // 2][:, i % 2, :] for i in range(S_TILES)]
+        ret_sb = [ret_pairs[i // 2][:, i % 2, :] for i in range(S_TILES)]
 
         def load_planes(planes, scale_rows, passes):
             for quadrant in range(4):
@@ -71,10 +73,13 @@ def tile_retnet_pc_kernel(tc, x, wg_words, wg_scales, ret, wo_words, wo_scales, 
                 )
 
         def load_x(i):
-            nc.sync.dma_start(out=x_sb[i][:], in_=x_rows[P * i : P * (i + 1), :])
+            nc.sync.dma_start(out=x_sb[i], in_=x_rows[P * i : P * (i + 1), :])
 
         def load_ret(i):
-            nc.sync.dma_start(out=ret_sb[i][:], in_=ret_rows[P * i : P * (i + 1), :])
+            nc.sync.dma_start(out=ret_sb[i], in_=ret_rows[P * i : P * (i + 1), :])
+
+        def load_pair(pair, rows, j):
+            nc.sync.dma_start(out=pair[:], in_=rows[2 * P * j : 2 * P * (j + 1), :].rearrange("(i p) c -> p i c", i=2))
 
         load_x(0)
         nc.vector.memset(wg_planes[:].bitcast(I32), 0)
@@ -107,21 +112,16 @@ def tile_retnet_pc_kernel(tc, x, wg_words, wg_scales, ret, wo_words, wo_scales, 
         load_wg(1)
         load_wg(2)
         load_wg(3)
-        load_x(2)
-        load_x(3)
+        load_pair(x_pairs[1], x_rows, 1)
         load_ret(1)
         load_ret(2)
         load_planes(wo_planes, wo_scales, H_PASSES)
         load_wo()
         load_ret(3)
-        load_x(4)
-        load_ret(4)
-        load_x(5)
-        load_ret(5)
-        load_x(6)
-        load_ret(6)
-        load_x(7)
-        load_ret(7)
+        load_pair(x_pairs[2], x_rows, 2)
+        load_pair(ret_pairs[2], ret_rows, 2)
+        load_pair(x_pairs[3], x_rows, 3)
+        load_pair(ret_pairs[3], ret_rows, 3)
         x_bank, x_grouped, x_codes, x_scales = {}, {}, {}, {}
         silu, h_sb = {}, {}
         h_banks, h_grouped, h_codes, h_scales, out_banks = {}, {}, {}, {}, {}
@@ -133,7 +133,7 @@ def tile_retnet_pc_kernel(tc, x, wg_words, wg_scales, ret, wo_words, wo_scales, 
 
         def transpose_x(i):
             x_bank[i] = psum.tile([P, 2, 2, P], F32, tag="xt", name="xt")
-            transpose_two_passes(nc, x_bank[i], x_sb[i][:].bitcast(F32), 0, ident, 2)
+            transpose_two_passes(nc, x_bank[i], x_sb[i].bitcast(F32), 0, ident, 2)
 
         def regroup_x(i):
             x_grouped[i] = work.tile([P, X_PASSES, P, 4], BF16, tag="x_grouped", align_bytes=256, name="x_grouped")
@@ -255,7 +255,7 @@ def tile_retnet_pc_kernel(tc, x, wg_words, wg_scales, ret, wo_words, wo_scales, 
         last = S_TILES - 1
 
         def ready_columns(r):
-            return [0,8,17,26,36,45,54,64][r]
+            return HEADS + HEADS * last * (r - 1) // (last - 1)
 
         keep_tensor_busy(4, "o", 2)
         transpose_x(0)
@@ -302,16 +302,16 @@ def tile_retnet_pc_kernel(tc, x, wg_words, wg_scales, ret, wo_words, wo_scales, 
             if r == 2:
                 quantise_x(3)
             first, end = ready_columns(r), ready_columns(r + 1)
-            on_vector = [1,1,1,1,1][r - 2]
+            on_vector = 2 - r % 2
             mean_square_on_vector(range(first, first + on_vector))
             squares = list(range(first + on_vector, end))
-            mean_square_on_scalar(squares[:[4,4,4,4,4][r - 2]])
+            mean_square_on_scalar(squares[:3])
             for n in range(early, G_BANKS):
                 gate_matmul(r, n)
             gate_times_norm(r - 1, range(HEADS))
             for n in range(OUT_BANKS):
                 out_matmul(r - 2, n)
-            mean_square_on_scalar(squares[[4,4,4,4,4][r - 2]:])
+            mean_square_on_scalar(squares[3:])
             if r > 2:
                 regroup_x(r + 1)
             if r + 1 < last:

@@ -303,12 +303,13 @@ def tile_retnet_pc_kernel(tc, x, wg_words, wg_scales, ret, wo_words, wo_scales, 
                 quantise_x(3)
             first, end = ready_columns(r), ready_columns(r + 1)
             on_vector = 2 - r % 2
-            mean_square_on_vector(range(first, first + on_vector))
+            mean_square_on_vector((first,))
             squares = list(range(first + on_vector, end))
             mean_square_on_scalar(squares[:3])
             for n in range(early, G_BANKS):
                 gate_matmul(r, n)
             gate_times_norm(r - 1, range(HEADS))
+            mean_square_on_vector(range(first + 1, first + on_vector))
             for n in range(OUT_BANKS):
                 out_matmul(r - 2, n)
             mean_square_on_scalar(squares[3:])

import concourse.mybir as mybir
from concourse.masks import make_identity

F32 = mybir.dt.float32
BF16 = mybir.dt.bfloat16
I32 = mybir.dt.int32
U32 = mybir.dt.uint32
U8 = mybir.dt.uint8
FP8X4 = mybir.dt.float8_e4m3fn_x4
ACT = mybir.ActivationFunctionType
ALU = mybir.AluOpType

P = 128
S, E, V = 1024, 1024, 2048
HEADS, HEAD_DIM = 8, 256
EPS = 1e-5
K_PASS = 512
N_TILE = 512
S_TILES = S // P
X_PASSES = E // K_PASS
H_PASSES = V // K_PASS
G_BANKS = V // N_TILE
OUT_BANKS = E // N_TILE
WORDS = K_PASS // 2
HALF = HEADS // 2

FLOPS = 2 * S * E * V + 2 * S * V * E


def transpose_two_passes(nc, bank, words, first_pass, ident, word_step):
    for g in range(2):
        start = WORDS * (first_pass + g)
        for u in range(2):
            first = start + (u if word_step == 2 else P * u)
            nc.tensor.transpose(bank[:, g, u, :], words[:, first : first + word_step * (P - 1) + 1 : word_step], ident[:])


def regroup_two_passes(copy, grouped, bank):
    copy(out=grouped.bitcast(F32), in_=bank[:].rearrange("p g u s -> p g s u"))


def quantise_two_passes(nc, codes, scales, grouped):
    nc.vector.quantize_mx(
        out=codes.rearrange("p g s -> p (g s)").bitcast(FP8X4),
        scales=scales.rearrange("p g s -> p (g s)"),
        in_=grouped.rearrange("p g s t -> p (g s t)"),
    )


def tile_retnet_pc_kernel(tc, x, wg_words, wg_scales, ret, wo_words, wo_scales, out):
    nc = tc.nc
    x_rows = x.flatten_outer_dims()
    ret_rows = ret.rearrange("b s h d -> (b s) (h d)")
    out_rows = out.flatten_outer_dims()

    with tc.tile_pool(name="keep", bufs=1) as keep, tc.tile_pool(name="work", bufs=3) as work, tc.psum_pool(
        name="psum", bufs=1
    ) as psum, tc.manual_schedule():
        wg_planes = keep.tile([P, V], U8, align_bytes=256)
        wo_planes = keep.tile([P, E], U8, align_bytes=256)
        wg_codes = keep.tile([P, X_PASSES, V], U32, align_bytes=256)
        wo_codes = keep.tile([P, H_PASSES, E], U32, align_bytes=256)
        x_pairs = [keep.tile([P, 2, E], BF16, name="x_pair%d" % j) for j in range(S_TILES // 2)]
        ret_pairs = [keep.tile([P, 2, V], BF16, name="ret_pair%d" % j) for j in range(S_TILES // 2)]
        x_sb = [x_pairs[i // 2][:, i % 2, :] for i in range(S_TILES)]
        ret_sb = [ret_pairs[i // 2][:, i % 2, :] for i in range(S_TILES)]

        def load_planes(planes, scale_rows, passes):
            for quadrant in range(4):
                nc.sync.dma_start(
                    out=planes[32 * quadrant : 32 * quadrant + 4 * passes, :].bitcast(I32),
                    in_=scale_rows[:, 4 * quadrant : 4 * quadrant + 4, :].bitcast(I32),
                )

        def load_x(i):
            nc.sync.dma_start(out=x_sb[i], in_=x_rows[P * i : P * (i + 1), :])

        def load_ret(i):
            nc.sync.dma_start(out=ret_sb[i], in_=ret_rows[P * i : P * (i + 1), :])

        def load_pair(pair, rows, j):
            nc.sync.dma_start(out=pair[:], in_=rows[2 * P * j : 2 * P * (j + 1), :].rearrange("(i p) c -> p i c", i=2))

        load_x(0)
        nc.vector.memset(wg_planes[:].bitcast(I32), 0)
        nc.vector.memset(wo_planes[:].bitcast(I32), 0)
        minus_half = keep.tile([P, 2 * HEADS], F32)
        nc.vector.memset(minus_half[:], -0.5)
        ones = keep.tile([P, N_TILE], BF16)
        nc.gpsimd.memset(ones[:], 1.0)
        ident = keep.tile([P, P], F32)
        make_identity(nc, ident[:])
        warm = keep.tile([P, 1], F32)
        nc.scalar.activation(out=warm[:], in_=minus_half[:, 0:1], func=ACT.Silu)
        def load_wg(n):
            cols = slice(N_TILE * n, N_TILE * (n + 1))
            nc.sync.dma_start(
                out=wg_codes[:, :, cols].bitcast(I32),
                in_=wg_words.bitcast(I32).rearrange("g p n t -> p g (n t)")[:, :, cols],
            )

        def load_wo():
            for g in range(H_PASSES):
                nc.sync.dma_start(
                    out=wo_codes[:, g, :].bitcast(I32), in_=wo_words[g].rearrange("p n t -> p (n t)").bitcast(I32)
                )

        load_planes(wg_planes, wg_scales, X_PASSES)
        load_x(1)
        load_ret(0)
        load_wg(0)
        load_wg(1)
        load_wg(2)
        load_wg(3)
        load_pair(x_pairs[1], x_rows, 1)
        load_ret(1)
        load_ret(2)
        load_planes(wo_planes, wo_scales, H_PASSES)
        load_wo()
        load_ret(3)
        load_pair(x_pairs[2], x_rows, 2)
        load_pair(ret_pairs[2], ret_rows, 2)
        load_pair(x_pairs[3], x_rows, 3)
        load_pair(ret_pairs[3], ret_rows, 3)
        x_bank, x_grouped, x_codes, x_scales = {}, {}, {}, {}
        silu, h_sb = {}, {}
        h_banks, h_grouped, h_codes, h_scales, out_banks = {}, {}, {}, {}, {}

        def keep_tensor_busy(count, tag, bufs):
            unread = psum.tile([P, N_TILE], F32, tag=tag, bufs=bufs, name="unread")
            for turn in range(count):
                nc.tensor.matmul(unread[:], lhsT=ones[:, :P], rhs=ones[:], start=True, stop=True)

        def transpose_x(i):
            x_bank[i] = psum.tile([P, 2, 2, P], F32, tag="xt", name="xt")
            transpose_two_passes(nc, x_bank[i], x_sb[i].bitcast(F32), 0, ident, 2)

        def regroup_x(i):
            x_grouped[i] = work.tile([P, X_PASSES, P, 4], BF16, tag="x_grouped", align_bytes=256, name="x_grouped")
            regroup_two_passes(nc.vector.tensor_copy, x_grouped[i][:], x_bank[i])

        def quantise_x(i):
            x_codes[i] = work.tile([P, X_PASSES, P], U32, tag="x_codes", bufs=5, align_bytes=256, name="x_codes")
            x_scales[i] = work.tile([P, X_PASSES, P], U8, tag="x_scales", bufs=5, align_bytes=256, name="x_scales")
            quantise_two_passes(nc, x_codes[i][:], x_scales[i][:], x_grouped[i][:])

        mean_sq = keep.tile([P, HEADS * S_TILES], F32)
        rstd = keep.tile([P, HEADS * S_TILES], F32)

        def head_of_ret(column):
            head = column % HEADS
            return ret_sb[column // HEADS][:, HEAD_DIM * head : HEAD_DIM * (head + 1)]

        def mean_square_on_scalar(columns):
            for column in columns:
                squares = work.tile([P, HEAD_DIM], BF16, tag="squares")
                nc.scalar.activation(
                    out=squares[:],
                    in_=head_of_ret(column),
                    func=ACT.Square,
                    scale=HEAD_DIM ** -0.5,
                    accum_out=mean_sq[:, column : column + 1],
                )

        def mean_square_on_vector(columns):
            for column in columns:
                squares = work.tile([P, HEAD_DIM], BF16, tag="squares_v")
                nc.vector.scalar_tensor_tensor(
                    out=squares[:],
                    in0=head_of_ret(column),
                    scalar=1.0 / HEAD_DIM,
                    in1=head_of_ret(column),
                    op0=ALU.mult,
                    op1=ALU.mult,
                    accum_out=mean_sq[:, column : column + 1],
                )

        def inverse_root(first, end):
            cols = slice(first, end)
            shifted = work.tile([P, end - first], F32, tag="shifted")
            nc.vector.tensor_scalar(out=shifted[:], in0=mean_sq[:, cols], scalar1=EPS, scalar2=None, op0=ALU.add)
            nc.gpsimd.tensor_tensor(out=rstd[:, cols], in0=shifted[:], in1=minus_half[:, : end - first], op=ALU.pow)

        def gate_matmul(i, n):
            cols = slice(N_TILE * n, N_TILE * (n + 1))
            acc = psum.tile([P, N_TILE], F32, tag="g", bufs=3)
            for g in range(X_PASSES):
                nc.tensor.matmul_mx(
                    out=acc[:],
                    lhsT=x_codes[i][:, g, :].bitcast(FP8X4),
                    lhsT_scale=x_scales[i][:, g, :],
                    rhs=wg_codes[:, g, cols].bitcast(FP8X4),
                    rhs_scale=wg_planes[4 * g : P, cols],
                    start=(g == 0),
                    stop=(g == X_PASSES - 1),
                )
            if n == 0:
                silu[i] = work.tile([P, V], F32, tag="silu", bufs=5, name="silu")
            nc.scalar.activation(out=silu[i][:, cols], in_=acc[:], func=ACT.Silu)

        def gate_times_norm(i, heads):
            if i not in h_sb:
                h_sb[i] = work.tile([P, V], BF16, tag="h_sb", name="h_sb")
            for head in heads:
                cols = slice(HEAD_DIM * head, HEAD_DIM * (head + 1))
                silu_words = silu[i][:, cols].rearrange("s (p u e) -> s u p e", u=2, e=2)
                ret_words = ret_sb[i][:, cols].rearrange("s (p u e) -> s u p e", u=2, e=2)
                for u in range(2):
                    start = K_PASS * (head // 2) + HEAD_DIM * u + P * (head % 2)
                    nc.vector.scalar_tensor_tensor(
                        out=h_sb[i][:, start : start + P].rearrange("s (p e) -> s p e", e=2),
                        in0=silu_words[:, u],
                        scalar=rstd[:, HEADS * i + head : HEADS * i + head + 1],
                        in1=ret_words[:, u],
                        op0=ALU.mult,
                        op1=ALU.mult,
                    )

        def transpose_h(i, half):
            h_banks[i, half] = psum.tile([P, 2, 2, P], F32, tag="ht", bufs=2, name="ht")
            transpose_two_passes(nc, h_banks[i, half], h_sb[i][:].bitcast(F32), 2 * half, ident, 1)

        def regroup_h(i, half, copy=nc.vector.tensor_copy):
            if i not in h_grouped:
                h_grouped[i] = work.tile([P, H_PASSES, P, 4], BF16, tag="h_grouped", align_bytes=256, name="h_grouped")
            regroup_two_passes(copy, h_grouped[i][:, 2 * half : 2 * half + 2], h_banks[i, half])

        def quantise_h(i, half):
            if i not in h_codes:
                h_codes[i] = work.tile([P, H_PASSES, P], U32, tag="h_codes", bufs=4, align_bytes=256, name="h_codes")
                h_scales[i] = work.tile([P, H_PASSES, P], U8, tag="h_scales", bufs=4, align_bytes=256, name="h_scales")
            two = slice(2 * half, 2 * half + 2)
            quantise_two_passes(nc, h_codes[i][:, two], h_scales[i][:, two], h_grouped[i][:, two])

        def out_matmul(i, n, passes=range(H_PASSES), tag="o", bufs=2, width=N_TILE):
            cols = slice(width * n, width * (n + 1))
            if (i, n, width) not in out_banks:
                out_banks[i, n, width] = psum.tile([P, N_TILE], F32, tag=tag, bufs=bufs, name="o")
            for g in passes:
                nc.tensor.matmul_mx(
                    out=out_banks[i, n, width][:, :width],
                    lhsT=h_codes[i][:, g, :].bitcast(FP8X4),
                    lhsT_scale=h_scales[i][:, g, :],
                    rhs=wo_codes[:, g, cols].bitcast(FP8X4),
                    rhs_scale=wo_planes[4 * g : P, cols],
                    start=(g == 0),
                    stop=(g == H_PASSES - 1),
                )

        def store_out(i, n, copy=nc.scalar.copy, width=N_TILE):
            result = work.tile([P, N_TILE], F32, tag="result", bufs=8)
            copy(out=result[:, :width], in_=out_banks[i, n, width][:, :width])
            nc.sync.dma_start(out=out_rows[P * i : P * (i + 1), width * n : width * (n + 1)], in_=result[:, :width])

        last = S_TILES - 1

        def ready_columns(r):
            return HEADS + HEADS * last * (r - 1) // (last - 1)

        keep_tensor_busy(4, "o", 2)
        transpose_x(0)
        regroup_x(0)
        keep_tensor_busy(2, "o", 2)
        transpose_x(1)
        quantise_x(0)
        mean_square_on_scalar(range(HALF))
        regroup_x(1)
        mean_square_on_vector((4,))
        quantise_x(1)
        mean_square_on_vector((5,))
        inverse_root(0, HALF)
        mean_square_on_vector((6, 7))
        inverse_root(HALF, HEADS)
        keep_tensor_busy(2, "o", 2)
        for n in range(G_BANKS):
            gate_matmul(0, n)
            gate_matmul(1, n)
            if n < G_BANKS - 1:
                gate_times_norm(0, (2 * n, 2 * n + 1))
        transpose_x(2)
        keep_tensor_busy(2, "o", 2)
        gate_times_norm(0, (6,))
        regroup_x(2)
        gate_times_norm(0, (7,))
        quantise_x(2)
        mean_square_on_scalar(range(HEADS + 2, ready_columns(2)))
        mean_square_on_vector(range(HEADS, HEADS + 2))
        inverse_root(HEADS, ready_columns(2))
        for r in range(2, last):
            early = 1 if r == 3 else 0
            for n in range(early):
                gate_matmul(r, n)
            transpose_h(r - 2, 0)
            transpose_h(r - 2, 1)
            transpose_x(r + 1)
            regroup_h(r - 2, 0)
            regroup_h(r - 2, 1)
            if r == 2:
                regroup_x(3)
            quantise_h(r - 2, 0)
            quantise_h(r - 2, 1)
            if r == 2:
                quantise_x(3)
            first, end = ready_columns(r), ready_columns(r + 1)
            on_vector = 2 - r % 2
            mean_square_on_vector((first,))
            squares = list(range(first + on_vector, end))
            mean_square_on_scalar(squares[:3])
            for n in range(early, G_BANKS):
                gate_matmul(r, n)
            gate_times_norm(r - 1, range(HEADS))
            mean_square_on_vector(range(first + 1, first + on_vector))
            for n in range(OUT_BANKS):
                out_matmul(r - 2, n)
            mean_square_on_scalar(squares[3:])
            if r > 2:
                regroup_x(r + 1)
            if r + 1 < last:
                inverse_root(first, end)
            if r > 2:
                quantise_x(r + 1)
            if r + 1 == last:
                inverse_root(first, end)
            store_out(r - 2, 0)
            store_out(r - 2, 1)
        transpose_h(last - 2, 0)
        transpose_h(last - 2, 1)
        regroup_h(last - 2, 0)
        regroup_h(last - 2, 1)
        quantise_h(last - 2, 0)
        quantise_h(last - 2, 1)
        for n in range(G_BANKS):
            gate_matmul(last, n)
        gate_times_norm(last - 1, range(HEADS))
        out_matmul(last - 2, 0)
        transpose_h(last - 1, 0)
        transpose_h(last - 1, 1)
        regroup_h(last - 1, 0, nc.scalar.copy)
        regroup_h(last - 1, 1, nc.scalar.copy)
        out_matmul(last - 2, 1)
        gate_times_norm(last, range(HALF))
        quantise_h(last - 1, 0)
        quantise_h(last - 1, 1)
        store_out(last - 2, 0)
        gate_times_norm(last, range(HALF, HEADS))
        out_matmul(last - 1, 0, tag="g", bufs=3)
        store_out(last - 2, 1)
        transpose_h(last, 0)
        transpose_h(last, 1)
        regroup_h(last, 0, nc.scalar.copy)
        regroup_h(last, 1)
        out_matmul(last - 1, 1, tag="g", bufs=3)
        store_out(last - 1, 0)
        quantise_h(last, 0)
        quantise_h(last, 1)
        store_out(last - 1, 1)
        half_bank = N_TILE // 2
        for n in range(4):
            out_matmul(last, n, range(0, 2), tag=("o", "g")[n // 2], bufs=2 + n // 2, width=half_bank)
        for n in range(4):
            out_matmul(last, n, range(2, H_PASSES), width=half_bank)
            store_out(last, n, (nc.scalar.copy, nc.vector.tensor_copy)[n % 2], half_bank)
